import numpy as np
import ml_dtypes


def mxq(x, axis, fmt="e4m3"):
    dtype, down = {"e4m3": (ml_dtypes.float8_e4m3fn, 7), "e5m2": (ml_dtypes.float8_e5m2, 14)}[fmt]
    v = np.moveaxis(np.asarray(x, np.float32).astype(ml_dtypes.bfloat16).astype(np.float64), axis, -1)
    blocks = v.reshape(v.shape[:-1] + (-1, 32))
    amax = np.abs(blocks).max(-1, keepdims=True)
    byte = np.maximum(np.where(amax > 0, np.frexp(amax)[1] - 1 + 127, 0) - down, 1)
    scale = np.exp2(byte - 127.0)
    codes = (blocks / scale).astype(np.float32).astype(dtype).astype(np.float64)
    return np.moveaxis((codes * scale).reshape(v.shape), -1, axis)


WIDE = False


def mx_kscale(k):
    if not WIDE:
        return np.ones(k)
    levels = np.array([10, -10, 5, -5, 0])
    if k % 512:
        return np.exp2(np.random.permutation(np.resize(levels, k // 32))).repeat(32)
    a = np.empty((k // 512, 16))
    for p in range(k // 512):
        a[p, :8] = np.random.permutation(np.resize(levels, 8))
        for g in range(8):
            far = levels[np.abs(levels - a[p, g]) >= 10]
            a[p, g + 8] = far[np.random.randint(len(far))]
    return np.exp2(a.ravel()).repeat(32)


BF16 = ml_dtypes.bfloat16


def bf(x):
    return np.asarray(x, np.float32).astype(BF16)


def f64(x):
    return np.asarray(x).astype(np.float64)


B, C, M, O, H, W = 4, 512, 512, 512, 32, 32
H2, W2 = H // 2, W // 2
KS = 3
PAD = KS // 2
BN_EPS = 1e-5


def haar_ll(x):
    a = x[:, :, 0::2, 0::2]
    b = x[:, :, 0::2, 1::2]
    c = x[:, :, 1::2, 0::2]
    d = x[:, :, 1::2, 1::2]
    return (a + b + c + d) * 0.5


def windows(u):
    up = np.pad(u, ((0, 0), (0, 0), (PAD, PAD), (PAD, PAD)))
    return np.stack([up[:, :, i:i + H2, j:j + W2] for i in range(KS) for j in range(KS)], axis=-1)


def setup_inputs():
    s, t = mx_kscale(C), mx_kscale(M)
    return {
        "x": bf(np.random.standard_normal((B, C, H, W)) * s[None, :, None, None]),
        "w_c1": bf(np.random.standard_normal((M, C)) / np.sqrt(C) * t[:, None] / s[None, :]),
        "b_c1": bf(np.random.standard_normal(M) * 0.3 * t),
        "w_q": bf(np.random.standard_normal((O, M)) / np.sqrt(M) / t[None, :]),
        "w_k": bf(np.random.standard_normal((O, M)) / np.sqrt(M) / t[None, :]),
        "w_v": bf(np.random.standard_normal((O, M)) / np.sqrt(M) / t[None, :]),
        "bn_gamma": bf(1.0 + 0.1 * np.random.standard_normal(O)),
        "bn_beta": bf(0.3 * np.random.standard_normal(O)),
        "prelu_a": bf(np.random.uniform(0.15, 0.35, (1,))),
    }


def reference(x, w_c1, b_c1, w_q, w_k, w_v, bn_gamma, bn_beta, prelu_a):
    ll = haar_ll(f64(x)).reshape(B, C, H2 * W2)
    y = (mxq(f64(w_c1), 1, "e4m3") @ mxq(ll, 1, "e4m3")) + f64(b_c1)[None, :, None]
    yq = mxq(y, 1, "e4m3")
    q = (mxq(f64(w_q), 1, "e4m3") @ yq).reshape(B, O, H2, W2)
    k = (mxq(f64(w_k), 1, "e4m3") @ yq).reshape(B, O, H2, W2)
    v = (mxq(f64(w_v), 1, "e4m3") @ yq).reshape(B, O, H2, W2)
    kw = windows(k)
    vw = windows(v)
    z = q[..., None] * kw
    e = np.exp(z - z.max(-1, keepdims=True))
    attn = e / e.sum(-1, keepdims=True)
    att = (attn * vw).sum(-1)
    m = att.mean(axis=(0, 2, 3), keepdims=True)
    var = att.var(axis=(0, 2, 3), keepdims=True)
    n = f64(bn_gamma)[None, :, None, None] * (att - m) / np.sqrt(var + BN_EPS) + f64(bn_beta)[None, :, None, None]
    return np.where(n >= 0, n, f64(prelu_a) * n)

@@ -1,0 +1,403 @@
+import concourse.mybir as mybir
+from concourse.masks import make_identity
+
+F32 = mybir.dt.float32
+BF16 = mybir.dt.bfloat16
+U32 = mybir.dt.uint32
+U8 = mybir.dt.uint8
+FP8X4 = mybir.dt.float8_e4m3fn_x4
+ALU = mybir.AluOpType
+ACT = mybir.ActivationFunctionType
+
+P = 128
+PACK = 4
+IMAGES = 4
+CHANNELS = 512
+SIDE = 16
+PIX = SIDE * SIDE
+PAIR = 2
+CHUNK = PAIR * PIX
+TILES = CHANNELS // P
+HALVES = IMAGES // PAIR
+CHUNKS = TILES * HALVES
+SHIFTS = (-1, 0, 1)
+TAPS = len(SHIFTS) * len(SHIFTS)
+BLOCKS = CHUNK // P
+BN_EPS = 1e-5
+BN_COUNT = IMAGES * PIX
+
+FLOPS = 4 * 2 * CHANNELS * CHANNELS * IMAGES * PIX
+
+
+def inside(shift):
+    return max(0, -shift), SIDE - max(0, shift)
+
+
+def tile_merge_pa_kernel(
+    tc, x, w_c1, b_c1, w_q, w_k, w_v, bn_gamma, bn_beta, prelu_a, out
+):
+    nc = tc.nc
+    weights = {"c1": w_c1, "q": w_q, "k": w_k, "v": w_v}
+
+    with tc.tile_pool(name="keep", bufs=1) as keep:
+        ident = keep.tile([P, P], F32)
+        make_identity(nc, ident[:])
+
+        w_codes = {}
+        w_scales = {}
+        for name in weights:
+            w_codes[name] = keep.tile([P, CHANNELS], U32, name="codes_" + name, align_bytes=64)
+            w_scales[name] = keep.tile([P, CHANNELS], U8, name="scales_" + name, align_bytes=64)
+        y_codes = keep.tile([P, IMAGES * PIX], U32, align_bytes=64)
+        y_scales = keep.tile([P, IMAGES * PIX], U8, align_bytes=64)
+
+        z_even = keep.tile([P, len(SHIFTS), len(SHIFTS), PAIR, SIDE, SIDE], F32)
+        z_odd = keep.tile([P, len(SHIFTS), len(SHIFTS), PAIR, SIDE, SIDE], F32)
+        pv = keep.tile([P, len(SHIFTS), len(SHIFTS), PAIR, SIDE, SIDE], F32)
+        for planes in (z_even, z_odd, pv):
+            nc.vector.memset(planes[:, 0, :, :, 0, :], 0.0)
+            nc.vector.memset(planes[:, 2, :, :, SIDE - 1, :], 0.0)
+            nc.vector.memset(planes[:, :, 0, :, :, 0], 0.0)
+            nc.vector.memset(planes[:, :, 2, :, :, SIDE - 1], 0.0)
+
+        bias_c1 = keep.tile([P, PACK], F32)
+        gamma_pm = keep.tile([P, TILES, 2], F32)
+        beta_pm = keep.tile([P, TILES, 2], F32)
+        minus_slope = keep.tile([P, 1], F32)
+        minus_half = keep.tile([P, 1], F32)
+        nc.vector.memset(minus_half[:], -0.5)
+        eps = keep.tile([P, 1], F32)
+        nc.vector.memset(eps[:], BN_EPS)
+
+        with tc.tile_pool(name="head", bufs=2) as head, tc.psum_pool(name="head_banks", bufs=4) as head_banks:
+            x_sb = []
+            w_raw = {}
+
+            def load_image(b):
+                x_sb.append(head.tile([P, PACK * 4 * PIX], BF16, name="x%d" % b, bufs=1))
+                nc.sync.dma_start(
+                    out=x_sb[b][:],
+                    in_=x[b].rearrange("(p t) h w -> p (t h w)", t=PACK),
+                )
+
+            def load_weight(name):
+                w_raw[name] = head.tile([P, TILES * CHANNELS], BF16, name="raw_" + name, bufs=1)
+                nc.sync.dma_start(out=w_raw[name][:], in_=weights[name].rearrange("(r a) k -> r (a k)", a=TILES))
+
+            load_image(0)
+            load_weight("c1")
+            for b in range(1, IMAGES):
+                load_image(b)
+            for name in ("q", "k", "v"):
+                load_weight(name)
+
+            b1_bf = head.tile([P, PACK], BF16, bufs=1)
+            nc.scalar.dma_start(out=b1_bf[:], in_=b_c1.rearrange("(r t) -> r t", t=PACK))
+            gamma_bf = head.tile([P, TILES], BF16, bufs=1)
+            nc.scalar.dma_start(out=gamma_bf[:], in_=bn_gamma.rearrange("(r a) -> r a", a=TILES))
+            beta_bf = head.tile([P, TILES], BF16, bufs=1)
+            nc.scalar.dma_start(out=beta_bf[:], in_=bn_beta.rearrange("(r a) -> r a", a=TILES))
+            slope_bf = head.tile([P, 1], BF16, bufs=1)
+            nc.scalar.dma_start(out=slope_bf[:], in_=prelu_a.partition_broadcast(P))
+
+            nc.vector.tensor_copy(out=bias_c1[:], in_=b1_bf[:])
+            nc.vector.tensor_copy(out=gamma_pm[:, :, 0], in_=gamma_bf[:])
+            nc.vector.tensor_scalar_mul(out=gamma_pm[:, :, 1], in0=gamma_bf[:], scalar1=-1.0)
+            nc.vector.tensor_copy(out=beta_pm[:, :, 0], in_=beta_bf[:])
+            nc.vector.tensor_scalar_mul(out=beta_pm[:, :, 1], in0=beta_bf[:], scalar1=-1.0)
+            nc.vector.tensor_scalar_mul(out=minus_slope[:], in0=slope_bf[:], scalar1=-1.0)
+
+            def quantise_weight(name):
+                words = w_raw[name][:].bitcast(F32)
+                grouped = head.tile([P, TILES * P * PACK], BF16, tag="grouped", align_bytes=64)
+                grouped_words = grouped[:].bitcast(F32).rearrange("p (a r u) -> p a r u", a=TILES, u=2)
+                for first in range(0, TILES, 2):
+                    turned = head_banks.tile([P, 2, 2, P], F32, tag="turned")
+                    for a in range(2):
+                        for u in range(2):
+                            row = (first + a) * 2 * P
+                            nc.tensor.transpose(
+                                turned[:, a, u, :], words[:, row + u : row + 2 * P : 2], ident[:]
+                            )
+                    nc.scalar.copy(
+                        out=grouped_words[:, first : first + 2],
+                        in_=turned[:].rearrange("p a u r -> p a r u"),
+                    )
+                nc.vector.quantize_mx(
+                    out=w_codes[name][:].bitcast(FP8X4), scales=w_scales[name][:], in_=grouped[:]
+                )
+
+            quantise_weight("c1")
+
+            ll_codes = head.tile([P, IMAGES * PIX], U32, bufs=1, align_bytes=64)
+            ll_scales = head.tile([P, IMAGES * PIX], U8, bufs=1, align_bytes=64)
+            for b in range(IMAGES):
+                row_pairs = x_sb[b][:].rearrange("p (r two w) -> p r two w", two=2, w=2 * SIDE)
+                row_sums = head.tile([P, PACK * PIX * 2], F32, tag="row_sums")
+                nc.vector.tensor_tensor(
+                    out=row_sums[:].rearrange("p (r w) -> p r w", w=2 * SIDE),
+                    in0=row_pairs[:, :, 0, :],
+                    in1=row_pairs[:, :, 1, :],
+                    op=ALU.add,
+                )
+                col_pairs = row_sums[:].rearrange("p (t x two) -> p x t two", t=PACK, two=2)
+                ll2 = head.tile([P, PIX, PACK], BF16, tag="ll2", align_bytes=64)
+                nc.vector.tensor_tensor(
+                    out=ll2[:], in0=col_pairs[:, :, :, 0], in1=col_pairs[:, :, :, 1], op=ALU.add
+                )
+                cols = slice(b * PIX, (b + 1) * PIX)
+                nc.vector.quantize_mx(
+                    out=ll_codes[:, cols].bitcast(FP8X4),
+                    scales=ll_scales[:, cols],
+                    in_=ll2[:].rearrange("p x t -> p (x t)"),
+                )
+
+            for name in ("q", "k", "v"):
+                quantise_weight(name)
+
+            y_bf = head.tile([P, IMAGES * PIX, PACK], BF16, bufs=1, align_bytes=64)
+            for g in range(IMAGES * PIX // P):
+                cols = slice(g * P, (g + 1) * P)
+                y_bank = head_banks.tile([P, PACK, P], F32, tag="y_bank")
+                for t in range(PACK):
+                    rows = slice(t * P, (t + 1) * P)
+                    nc.tensor.matmul_mx(
+                        out=y_bank[:, t, :],
+                        lhsT=w_codes["c1"][:, rows].bitcast(FP8X4),
+                        lhsT_scale=w_scales["c1"][:, rows],
+                        rhs=ll_codes[:, cols].bitcast(FP8X4),
+                        rhs_scale=ll_scales[:, cols],
+                        start=True,
+                        stop=True,
+                    )
+                nc.vector.scalar_tensor_tensor(
+                    out=y_bf[:, cols, :],
+                    in0=y_bank[:].rearrange("p t x -> p x t"),
+                    scalar=0.5,
+                    in1=bias_c1[:].unsqueeze(1).to_broadcast([P, P, PACK]),
+                    op0=ALU.mult,
+                    op1=ALU.add,
+                )
+            for h in range(HALVES):
+                cols = slice(h * CHUNK, (h + 1) * CHUNK)
+                nc.vector.quantize_mx(
+                    out=y_codes[:, cols].bitcast(FP8X4),
+                    scales=y_scales[:, cols],
+                    in_=y_bf[:, cols, :].rearrange("p x t -> p (x t)"),
+                )
+
+        z_pair = (z_even, z_odd)
+        pv_blocks = pv[:].rearrange("p s t b (f i) j -> p (s t) (b f) (i j)", f=2)
+        out_tiles = out.rearrange("b (r a) h w -> a r b (h w)", a=TILES)
+        q_of, k_of, v_of, e_of, den_of, num_of = {}, {}, {}, {}, {}, {}
+        r_den_of, att_of, sums_of, mean_of, var_of, r_std_of, above_of, below_of = {}, {}, {}, {}, {}, {}, {}, {}
+
+        with tc.tile_pool(name="work", bufs=2) as work, tc.psum_pool(name="banks", bufs=2) as banks, tc.manual_schedule():
+
+            def project(name, c, tag, bufs):
+                a, h = divmod(c, HALVES)
+                bank = banks.tile([P, PAIR, SIDE, SIDE], F32, tag=tag, bufs=bufs)
+                rows = slice(a * P, (a + 1) * P)
+                cols = slice(h * CHUNK, (h + 1) * CHUNK)
+                nc.tensor.matmul_mx(
+                    out=bank[:].rearrange("p b i j -> p (b i j)"),
+                    lhsT=w_codes[name][:, rows].bitcast(FP8X4),
+                    lhsT_scale=w_scales[name][:, rows],
+                    rhs=y_codes[:, cols].bitcast(FP8X4),
+                    rhs_scale=y_scales[:, cols],
+                    start=True,
+                    stop=True,
+                )
+                return bank
+
+            def project_qk(c):
+                q_bank = project("q", c, "short", 2)
+                k_of[c] = project("k", c, "bank_k", 1)
+                q_sb = work.tile([P, PAIR, SIDE, SIDE], F32, tag="q_sb")
+                nc.scalar.copy(out=q_sb[:], in_=q_bank[:])
+                q_of[c] = q_sb
+
+            def project_v(c):
+                v_of[c] = project("v", c, "bank_v", 1)
+
+            def times_neighbours(planes, bank, maps):
+                for s, di in enumerate(SHIFTS):
+                    i0, i1 = inside(di)
+                    for t, dj in enumerate(SHIFTS):
+                        j0, j1 = inside(dj)
+                        nc.vector.tensor_tensor(
+                            out=planes[:, s, t, :, i0:i1, j0:j1],
+                            in0=bank[:, :, i0 + di : i1 + di, j0 + dj : j1 + dj],
+                            in1=maps(s, t)[:, :, i0:i1, j0:j1],
+                            op=ALU.mult,
+                        )
+
+            def sum_planes(blocks, tag):
+                total = banks.tile([P, BLOCKS, P], F32, tag=tag)
+                for g in range(BLOCKS):
+                    for d in range(TAPS):
+                        nc.tensor.matmul(
+                            out=total[:, g, :],
+                            lhsT=blocks[:, d, g, :],
+                            rhs=ident[:],
+                            is_transpose=True,
+                            start=(d == 0),
+                            stop=(d == TAPS - 1),
+                        )
+                return total
+
+            def products(c):
+                times_neighbours(z_pair[c % 2], k_of[c], lambda s, t: q_of[c])
+
+            def stabilise(c):
+                z_planes = z_pair[c % 2][:].rearrange("p s t b i j -> p (s t) b (i j)")
+                top = work.tile([P, 4, PAIR, PIX], F32, tag="top")
+                z_max = work.tile([P, PAIR, PIX], F32, tag="z_max")
+                for b in range(PAIR):
+                    nc.vector.tensor_max(out=top[:, :, b], in0=z_planes[:, 0:4, b], in1=z_planes[:, 4:8, b])
+                for b in range(PAIR):
+                    nc.vector.tensor_max(out=top[:, 0:2, b], in0=top[:, 0:2, b], in1=top[:, 2:4, b])
+                for b in range(PAIR):
+                    nc.vector.tensor_max(out=top[:, 0, b], in0=top[:, 0, b], in1=top[:, 1, b])
+                for b in range(PAIR):
+                    nc.vector.tensor_max(out=z_max[:, b], in0=top[:, 0, b], in1=z_planes[:, 8, b])
+                e = work.tile([P, TAPS, PAIR, PIX], F32, tag="e")
+                for b in range(PAIR):
+                    nc.gpsimd.tensor_tensor(
+                        out=e[:, :, b],
+                        in0=z_planes[:, :, b],
+                        in1=z_max[:, b].unsqueeze(1).to_broadcast([P, TAPS, PIX]),
+                        op=ALU.subtract,
+                    )
+                    nc.scalar.activation(out=e[:, :, b], in_=e[:, :, b], func=ACT.Exp)
+                e_of[c] = e
+
+            def sum_e(c):
+                den_of[c] = sum_planes(e_of[c][:].rearrange("p d b (f x) -> p d (b f) x", f=2), "den_t")
+
+            def weigh(c):
+                e_maps = e_of[c][:].rearrange("p (s t) b (i j) -> p s t b i j", s=len(SHIFTS), i=SIDE)
+                times_neighbours(pv, v_of[c], lambda s, t: e_maps[:, s, t])
+                num_of[c] = sum_planes(pv_blocks, "num_t")
+
+            def reciprocal(a):
+                ln_den = work.tile([P, HALVES, BLOCKS, P], F32, tag="ln_den", bufs=1)
+                for h in range(HALVES):
+                    nc.scalar.activation(out=ln_den[:, h], in_=den_of[a * HALVES + h][:], func=ACT.Ln)
+                r_den = work.tile([P, HALVES, BLOCKS, P], F32, tag="r_den")
+                nc.scalar.activation(out=r_den[:], in_=ln_den[:], func=ACT.Exp, scale=-1.0)
+                r_den_of[a] = r_den
+
+            def divide(a):
+                att = work.tile([P, HALVES, CHUNK], F32, tag="att")
+                att_sums = work.tile([P, HALVES], F32, tag="att_sums")
+                for h in range(HALVES):
+                    att_t = work.tile([P, BLOCKS, P], F32, tag="att_t")
+                    nc.vector.tensor_mul(out=att_t[:], in0=num_of[a * HALVES + h][:], in1=r_den_of[a][:, h])
+                    att_bank = banks.tile([P, BLOCKS, P], F32, tag="short")
+                    for g in range(BLOCKS):
+                        nc.tensor.transpose(att_bank[:, g, :], att_t[:, g, :], ident[:])
+                    nc.scalar.activation(
+                        out=att[:, h, :],
+                        in_=att_bank[:].rearrange("p g x -> p (g x)"),
+                        func=ACT.Copy,
+                        accum_out=att_sums[:, h : h + 1],
+                    )
+                att_of[a], sums_of[a] = att, att_sums
+
+            def statistics(a):
+                parts = work.tile([P, HALVES], F32, tag="parts")
+                nc.scalar.activation(out=parts[:], in_=sums_of[a][:], func=ACT.Copy, scale=-1.0 / BN_COUNT)
+                minus_mean = work.tile([P, 1], F32, tag="minus_mean")
+                nc.scalar.activation(out=minus_mean[:], in_=parts[:, 0:1], func=ACT.Identity, bias=parts[:, 1:2])
+                squares = work.tile([P, HALVES * CHUNK], F32, tag="squares", bufs=1)
+                sum_squares = work.tile([P, 1], F32, tag="sum_squares")
+                nc.scalar.activation(
+                    out=squares[:],
+                    in_=att_of[a][:].rearrange("p h x -> p (h x)"),
+                    func=ACT.Square,
+                    bias=minus_mean[:],
+                    accum_out=sum_squares[:],
+                )
+                var_eps = work.tile([P, 1], F32, tag="var_eps")
+                nc.scalar.activation(
+                    out=var_eps[:], in_=sum_squares[:], func=ACT.Identity, scale=1.0 / BN_COUNT, bias=eps[:]
+                )
+                mean_of[a], var_of[a] = minus_mean, var_eps
+
+            def rsqrt(a):
+                r_std = work.tile([P, 1], F32, tag="r_std")
+                nc.gpsimd.tensor_tensor(out=r_std[:], in0=var_of[a][:], in1=minus_half[:], op=ALU.pow)
+                r_std_of[a] = r_std
+
+            def affine(a):
+                gain = work.tile([P, 2], F32, tag="gain")
+                nc.scalar.activation(out=gain[:], in_=gamma_pm[:, a, :], func=ACT.Copy, scale=r_std_of[a][:])
+                shift = work.tile([P, 2], F32, tag="shift")
+                for sign in range(2):
+                    nc.scalar.activation(
+                        out=shift[:, sign : sign + 1],
+                        in_=gain[:, sign : sign + 1],
+                        func=ACT.Identity,
+                        scale=mean_of[a][:],
+                        bias=beta_pm[:, a, sign : sign + 1],
+                    )
+                above = work.tile([P, HALVES, CHUNK], F32, tag="above")
+                below = work.tile([P, HALVES, CHUNK], F32, tag="below")
+                for h in range(HALVES):
+                    nc.scalar.activation(
+                        out=above[:, h], in_=att_of[a][:, h], func=ACT.Relu, scale=gain[:, 0:1], bias=shift[:, 0:1]
+                    )
+                    nc.scalar.activation(
+                        out=below[:, h], in_=att_of[a][:, h], func=ACT.Relu, scale=gain[:, 1:2], bias=shift[:, 1:2]
+                    )
+                above_of[a], below_of[a] = above, below
+
+            def finish(a):
+                result = work.tile([P, HALVES, CHUNK], F32, tag="result")
+                for h in range(HALVES):
+                    nc.vector.scalar_tensor_tensor(
+                        out=result[:, h],
+                        in0=below_of[a][:, h],
+                        scalar=minus_slope[:],
+                        in1=above_of[a][:, h],
+                        op0=ALU.mult,
+                        op1=ALU.add,
+                    )
+                    nc.sync.dma_start(
+                        out=out_tiles[a][:, h * PAIR : (h + 1) * PAIR, :],
+                        in_=result[:, h].rearrange("p (b x) -> p b x", b=PAIR),
+                    )
+
+            def live(c):
+                return 0 <= c < CHUNKS
+
+            def group_due(r, lag):
+                a, rest = divmod(r - lag, HALVES)
+                return a if rest == 0 and 0 <= a < TILES else None
+
+            project_qk(0)
+            for r in range(CHUNKS + 4):
+                if live(r):
+                    products(r)
+                if live(r + 1):
+                    project_qk(r + 1)
+                if group_due(r, 3) is not None:
+                    divide(group_due(r, 3))
+                    statistics(group_due(r, 3))
+                if live(r - 1):
+                    sum_e(r - 1)
+                if group_due(r, 4) is not None:
+                    affine(group_due(r, 4))
+                if group_due(r, 2) is not None:
+                    reciprocal(group_due(r, 2))
+                if group_due(r, 5) is not None:
+                    finish(group_due(r, 5))
+                if live(r):
+                    stabilise(r)
+                if live(r - 1):
+                    weigh(r - 1)
+                if live(r):
+                    project_v(r)
+                if group_due(r, 3) is not None:
+                    rsqrt(group_due(r, 3))

@@ -23,6 +23,7 @@ CHUNKS = TILES * HALVES
 SHIFTS = (-1, 0, 1)
 TAPS = len(SHIFTS) * len(SHIFTS)
 BLOCKS = CHUNK // P
+RUN = 4
 BN_EPS = 1e-5
 BN_COUNT = IMAGES * PIX
 
@@ -39,7 +40,7 @@ def tile_merge_pa_kernel(
     nc = tc.nc
     weights = {"c1": w_c1, "q": w_q, "k": w_k, "v": w_v}
 
-    with tc.tile_pool(name="keep", bufs=1) as keep:
+    with tc.tile_pool(name="keep", bufs=1) as keep, tc.manual_schedule():
         ident = keep.tile([P, P], F32)
         make_identity(nc, ident[:])
 
@@ -54,7 +55,8 @@ def tile_merge_pa_kernel(
         z_even = keep.tile([P, len(SHIFTS), len(SHIFTS), PAIR, SIDE, SIDE], F32)
         z_odd = keep.tile([P, len(SHIFTS), len(SHIFTS), PAIR, SIDE, SIDE], F32)
         pv = keep.tile([P, len(SHIFTS), len(SHIFTS), PAIR, SIDE, SIDE], F32)
-        for planes in (z_even, z_odd, pv):
+        nc.gpsimd.memset(pv[:], 0.0)
+        for planes in (z_even, z_odd):
             nc.vector.memset(planes[:, 0, :, :, 0, :], 0.0)
             nc.vector.memset(planes[:, 2, :, :, SIDE - 1, :], 0.0)
             nc.vector.memset(planes[:, :, 0, :, :, 0], 0.0)
@@ -65,51 +67,48 @@ def tile_merge_pa_kernel(
         beta_pm = keep.tile([P, TILES, 2], F32)
         minus_slope = keep.tile([P, 1], F32)
         minus_half = keep.tile([P, 1], F32)
-        nc.vector.memset(minus_half[:], -0.5)
+        nc.gpsimd.memset(minus_half[:], -0.5)
         eps = keep.tile([P, 1], F32)
-        nc.vector.memset(eps[:], BN_EPS)
+        nc.gpsimd.memset(eps[:], BN_EPS)
 
         with tc.tile_pool(name="head", bufs=2) as head, tc.psum_pool(name="head_banks", bufs=4) as head_banks:
             x_sb = []
             w_raw = {}
 
-            def load_image(b):
+            def load_image(b, parts):
                 x_sb.append(head.tile([P, PACK * 4 * PIX], BF16, name="x%d" % b, bufs=1))
-                nc.sync.dma_start(
-                    out=x_sb[b][:],
-                    in_=x[b].rearrange("(p t) h w -> p (t h w)", t=PACK),
-                )
+                step = PACK * 4 * PIX // parts
+                for part in range(parts):
+                    cols = slice(part * step, (part + 1) * step)
+                    nc.sync.dma_start(
+                        out=x_sb[b][:, cols], in_=x[b].rearrange("(p t) h w -> p (t h w)", t=PACK)[:, cols]
+                    )
 
             def load_weight(name):
                 w_raw[name] = head.tile([P, TILES * CHANNELS], BF16, name="raw_" + name, bufs=1)
                 nc.sync.dma_start(out=w_raw[name][:], in_=weights[name].rearrange("(r a) k -> r (a k)", a=TILES))
 
-            load_image(0)
+            load_image(0, 2)
             load_weight("c1")
-            for b in range(1, IMAGES):
-                load_image(b)
+            load_image(1, 1)
+            b1_bf = head.tile([P, PACK], BF16, bufs=1)
+            nc.sync.dma_start(out=b1_bf[:], in_=b_c1.rearrange("(r t) -> r t", t=PACK))
+            load_image(2, 1)
+            load_image(3, 1)
             for name in ("q", "k", "v"):
                 load_weight(name)
-
-            b1_bf = head.tile([P, PACK], BF16, bufs=1)
-            nc.scalar.dma_start(out=b1_bf[:], in_=b_c1.rearrange("(r t) -> r t", t=PACK))
             gamma_bf = head.tile([P, TILES], BF16, bufs=1)
-            nc.scalar.dma_start(out=gamma_bf[:], in_=bn_gamma.rearrange("(r a) -> r a", a=TILES))
+            nc.sync.dma_start(out=gamma_bf[:], in_=bn_gamma.rearrange("(r a) -> r a", a=TILES))
             beta_bf = head.tile([P, TILES], BF16, bufs=1)
-            nc.scalar.dma_start(out=beta_bf[:], in_=bn_beta.rearrange("(r a) -> r a", a=TILES))
+            nc.sync.dma_start(out=beta_bf[:], in_=bn_beta.rearrange("(r a) -> r a", a=TILES))
             slope_bf = head.tile([P, 1], BF16, bufs=1)
-            nc.scalar.dma_start(out=slope_bf[:], in_=prelu_a.partition_broadcast(P))
+            nc.sync.dma_start(out=slope_bf[:], in_=prelu_a.partition_broadcast(P))
 
-            nc.vector.tensor_copy(out=bias_c1[:], in_=b1_bf[:])
-            nc.vector.tensor_copy(out=gamma_pm[:, :, 0], in_=gamma_bf[:])
-            nc.vector.tensor_scalar_mul(out=gamma_pm[:, :, 1], in0=gamma_bf[:], scalar1=-1.0)
-            nc.vector.tensor_copy(out=beta_pm[:, :, 0], in_=beta_bf[:])
-            nc.vector.tensor_scalar_mul(out=beta_pm[:, :, 1], in0=beta_bf[:], scalar1=-1.0)
-            nc.vector.tensor_scalar_mul(out=minus_slope[:], in0=slope_bf[:], scalar1=-1.0)
+            grouped_of = {}
 
-            def quantise_weight(name):
+            def turn_weight(name):
                 words = w_raw[name][:].bitcast(F32)
-                grouped = head.tile([P, TILES * P * PACK], BF16, tag="grouped", align_bytes=64)
+                grouped = head.tile([P, TILES * P * PACK], BF16, name="grouped_" + name, bufs=1, align_bytes=64)
                 grouped_words = grouped[:].bitcast(F32).rearrange("p (a r u) -> p a r u", a=TILES, u=2)
                 for first in range(0, TILES, 2):
                     turned = head_banks.tile([P, 2, 2, P], F32, tag="turned")
@@ -123,40 +122,56 @@ def tile_merge_pa_kernel(
                         out=grouped_words[:, first : first + 2],
                         in_=turned[:].rearrange("p a u r -> p a r u"),
                     )
-                nc.vector.quantize_mx(
-                    out=w_codes[name][:].bitcast(FP8X4), scales=w_scales[name][:], in_=grouped[:]
-                )
+                grouped_of[name] = grouped
 
-            quantise_weight("c1")
+            def quantise_weight(name):
+                nc.vector.quantize_mx(
+                    out=w_codes[name][:].bitcast(FP8X4), scales=w_scales[name][:], in_=grouped_of[name][:]
+                )
 
             ll_codes = head.tile([P, IMAGES * PIX], U32, bufs=1, align_bytes=64)
             ll_scales = head.tile([P, IMAGES * PIX], U8, bufs=1, align_bytes=64)
-            for b in range(IMAGES):
-                row_pairs = x_sb[b][:].rearrange("p (r two w) -> p r two w", two=2, w=2 * SIDE)
-                row_sums = head.tile([P, PACK * PIX * 2], F32, tag="row_sums")
+            row_sums_of, ll2_of = {}, {}
+
+            def add_rows(b, part):
+                if part == 0:
+                    row_sums_of[b] = head.tile([P, PACK * PIX * 2], F32, name="row_sums", bufs=2)
+                half = PACK * PIX
+                row_pairs = x_sb[b][:, 2 * part * half : 2 * (part + 1) * half].rearrange(
+                    "p (r two w) -> p r two w", two=2, w=2 * SIDE
+                )
                 nc.vector.tensor_tensor(
-                    out=row_sums[:].rearrange("p (r w) -> p r w", w=2 * SIDE),
+                    out=row_sums_of[b][:, part * half : (part + 1) * half].rearrange("p (r w) -> p r w", w=2 * SIDE),
                     in0=row_pairs[:, :, 0, :],
                     in1=row_pairs[:, :, 1, :],
                     op=ALU.add,
                 )
-                col_pairs = row_sums[:].rearrange("p (t x two) -> p x t two", t=PACK, two=2)
-                ll2 = head.tile([P, PIX, PACK], BF16, tag="ll2", align_bytes=64)
+
+            def add_columns(b, part):
+                if part == 0:
+                    ll2_of[b] = head.tile([P, PIX, PACK], BF16, name="ll2", bufs=2, align_bytes=64)
+                pixels = slice(part * PIX // 2, (part + 1) * PIX // 2)
+                col_pairs = row_sums_of[b][:].rearrange("p (t x two) -> p t x two", t=PACK, two=2)[:, :, pixels, :]
+                col_pairs = col_pairs.rearrange("p t (c i) two -> p c t i two", i=RUN)
                 nc.vector.tensor_tensor(
-                    out=ll2[:], in0=col_pairs[:, :, :, 0], in1=col_pairs[:, :, :, 1], op=ALU.add
+                    out=ll2_of[b][:, pixels, :].rearrange("p (c i) t -> p c t i", i=RUN),
+                    in0=col_pairs[:, :, :, :, 0],
+                    in1=col_pairs[:, :, :, :, 1],
+                    op=ALU.add,
                 )
+
+            def quantise_ll(b):
                 cols = slice(b * PIX, (b + 1) * PIX)
                 nc.vector.quantize_mx(
                     out=ll_codes[:, cols].bitcast(FP8X4),
                     scales=ll_scales[:, cols],
-                    in_=ll2[:].rearrange("p x t -> p (x t)"),
+                    in_=ll2_of[b][:].rearrange("p x t -> p (x t)"),
                 )
 
-            for name in ("q", "k", "v"):
-                quantise_weight(name)
-
             y_bf = head.tile([P, IMAGES * PIX, PACK], BF16, bufs=1, align_bytes=64)
-            for g in range(IMAGES * PIX // P):
+            y_bank_of = {}
+
+            def multiply_y(g):
                 cols = slice(g * P, (g + 1) * P)
                 y_bank = head_banks.tile([P, PACK, P], F32, tag="y_bank")
                 for t in range(PACK):
@@ -170,15 +185,19 @@ def tile_merge_pa_kernel(
                         start=True,
                         stop=True,
                     )
+                y_bank_of[g] = y_bank
+
+            def add_bias(g):
                 nc.vector.scalar_tensor_tensor(
-                    out=y_bf[:, cols, :],
-                    in0=y_bank[:].rearrange("p t x -> p x t"),
+                    out=y_bf[:, g * P : (g + 1) * P, :],
+                    in0=y_bank_of[g][:].rearrange("p t x -> p x t"),
                     scalar=0.5,
                     in1=bias_c1[:].unsqueeze(1).to_broadcast([P, P, PACK]),
                     op0=ALU.mult,
                     op1=ALU.add,
                 )
-            for h in range(HALVES):
+
+            def quantise_y(h):
                 cols = slice(h * CHUNK, (h + 1) * CHUNK)
                 nc.vector.quantize_mx(
                     out=y_codes[:, cols].bitcast(FP8X4),
@@ -186,13 +205,49 @@ def tile_merge_pa_kernel(
                     in_=y_bf[:, cols, :].rearrange("p x t -> p (x t)"),
                 )
 
+            for b, name in enumerate(("c1", "q", "k", "v")):
+                add_rows(b, 0)
+                if b >= 1:
+                    quantise_ll(b - 1)
+                add_rows(b, 1)
+                if b == 1:
+                    quantise_weight("c1")
+                    nc.scalar.copy(out=bias_c1[:], in_=b1_bf[:])
+                if b >= 1:
+                    multiply_y(2 * b - 2)
+                    multiply_y(2 * b - 1)
+                if b >= 2:
+                    add_bias(2 * b - 4)
+                add_columns(b, 0)
+                if b >= 2:
+                    add_bias(2 * b - 3)
+                add_columns(b, 1)
+                turn_weight(name)
+            quantise_weight("q")
+            quantise_ll(3)
+            multiply_y(6)
+            multiply_y(7)
+            quantise_weight("k")
+            quantise_y(0)
+            add_bias(4)
+            add_bias(5)
+            quantise_weight("v")
+            add_bias(6)
+            add_bias(7)
+            quantise_y(1)
+            nc.scalar.copy(out=gamma_pm[:, :, 0], in_=gamma_bf[:])
+            nc.scalar.mul(out=gamma_pm[:, :, 1], in_=gamma_bf[:], mul=-1.0)
+            nc.scalar.copy(out=beta_pm[:, :, 0], in_=beta_bf[:])
+            nc.scalar.mul(out=beta_pm[:, :, 1], in_=beta_bf[:], mul=-1.0)
+            nc.scalar.mul(out=minus_slope[:], in_=slope_bf[:], mul=-1.0)
+
         z_pair = (z_even, z_odd)
         pv_blocks = pv[:].rearrange("p s t b (f i) j -> p (s t) (b f) (i j)", f=2)
         out_tiles = out.rearrange("b (r a) h w -> a r b (h w)", a=TILES)
         q_of, k_of, v_of, e_of, den_of, num_of = {}, {}, {}, {}, {}, {}
         r_den_of, att_of, sums_of, mean_of, var_of, r_std_of, above_of, below_of = {}, {}, {}, {}, {}, {}, {}, {}
 
-        with tc.tile_pool(name="work", bufs=2) as work, tc.psum_pool(name="banks", bufs=2) as banks, tc.manual_schedule():
+        with tc.tile_pool(name="work", bufs=2) as work, tc.psum_pool(name="banks", bufs=2) as banks:
 
             def project(name, c, tag, bufs):
                 a, h = divmod(c, HALVES)

@@ -66,6 +66,7 @@ def tile_merge_pa_kernel(
         gamma_pm = keep.tile([P, TILES, 2], F32)
         beta_pm = keep.tile([P, TILES, 2], F32)
         minus_slope = keep.tile([P, 1], F32)
+        slope_less_one = keep.tile([P, 1], F32)
         minus_half = keep.tile([P, 1], F32)
         nc.gpsimd.memset(minus_half[:], -0.5)
         eps = keep.tile([P, 1], F32)
@@ -240,11 +241,12 @@ def tile_merge_pa_kernel(
             nc.scalar.copy(out=beta_pm[:, :, 0], in_=beta_bf[:])
             nc.scalar.mul(out=beta_pm[:, :, 1], in_=beta_bf[:], mul=-1.0)
             nc.scalar.mul(out=minus_slope[:], in_=slope_bf[:], mul=-1.0)
+            nc.scalar.add(out=slope_less_one[:], in_=slope_bf[:], add=-1.0)
 
         z_pair = (z_even, z_odd)
         pv_blocks = pv[:].rearrange("p s t b (f i) j -> p (s t) (b f) (i j)", f=2)
         out_tiles = out.rearrange("b (r a) h w -> a r b (h w)", a=TILES)
-        q_of, k_of, v_of, e_of, den_of, num_of = {}, {}, {}, {}, {}, {}
+        q_of, k_of, v_of, z_max_of, e_of, den_of, num_of = {}, {}, {}, {}, {}, {}, {}
         r_den_of, att_of, sums_of, mean_of, var_of, r_std_of, above_of, below_of = {}, {}, {}, {}, {}, {}, {}, {}
 
         with tc.tile_pool(name="work", bufs=2) as work, tc.psum_pool(name="banks", bufs=2) as banks:
@@ -265,9 +267,11 @@ def tile_merge_pa_kernel(
                 )
                 return bank
 
-            def project_qk(c):
-                q_bank = project("q", c, "short", 2)
+            def project_k(c):
                 k_of[c] = project("k", c, "bank_k", 1)
+
+            def project_q(c):
+                q_bank = project("q", c, "short", 2)
                 q_sb = work.tile([P, PAIR, SIDE, SIDE], F32, tag="q_sb")
                 nc.scalar.copy(out=q_sb[:], in_=q_bank[:])
                 q_of[c] = q_sb
@@ -275,36 +279,35 @@ def tile_merge_pa_kernel(
             def project_v(c):
                 v_of[c] = project("v", c, "bank_v", 1)
 
-            def times_neighbours(planes, bank, maps):
+            def times_neighbours(planes, bank, maps, images=slice(0, PAIR)):
                 for s, di in enumerate(SHIFTS):
                     i0, i1 = inside(di)
                     for t, dj in enumerate(SHIFTS):
                         j0, j1 = inside(dj)
                         nc.vector.tensor_tensor(
-                            out=planes[:, s, t, :, i0:i1, j0:j1],
-                            in0=bank[:, :, i0 + di : i1 + di, j0 + dj : j1 + dj],
-                            in1=maps(s, t)[:, :, i0:i1, j0:j1],
+                            out=planes[:, s, t, images, i0:i1, j0:j1],
+                            in0=bank[:, images, i0 + di : i1 + di, j0 + dj : j1 + dj],
+                            in1=maps(s, t)[:, images, i0:i1, j0:j1],
                             op=ALU.mult,
                         )
 
-            def sum_planes(blocks, tag):
-                total = banks.tile([P, BLOCKS, P], F32, tag=tag)
+            def sum_planes(total, blocks, images=range(PAIR)):
                 for g in range(BLOCKS):
-                    for d in range(TAPS):
-                        nc.tensor.matmul(
-                            out=total[:, g, :],
-                            lhsT=blocks[:, d, g, :],
-                            rhs=ident[:],
-                            is_transpose=True,
-                            start=(d == 0),
-                            stop=(d == TAPS - 1),
-                        )
-                return total
+                    if g // (BLOCKS // PAIR) in images:
+                        for d in range(TAPS):
+                            nc.tensor.matmul(
+                                out=total[:, g, :],
+                                lhsT=blocks[:, d, g, :],
+                                rhs=ident[:],
+                                is_transpose=True,
+                                start=(d == 0),
+                                stop=(d == TAPS - 1),
+                            )
 
             def products(c):
                 times_neighbours(z_pair[c % 2], k_of[c], lambda s, t: q_of[c])
 
-            def stabilise(c):
+            def maxima(c):
                 z_planes = z_pair[c % 2][:].rearrange("p s t b i j -> p (s t) b (i j)")
                 top = work.tile([P, 4, PAIR, PIX], F32, tag="top")
                 z_max = work.tile([P, PAIR, PIX], F32, tag="z_max")
@@ -316,24 +319,39 @@ def tile_merge_pa_kernel(
                     nc.vector.tensor_max(out=top[:, 0, b], in0=top[:, 0, b], in1=top[:, 1, b])
                 for b in range(PAIR):
                     nc.vector.tensor_max(out=z_max[:, b], in0=top[:, 0, b], in1=z_planes[:, 8, b])
+                z_max_of[c] = z_max
+
+            def subtract(c, engines):
+                z_planes = z_pair[c % 2][:].rearrange("p s t b i j -> p (s t) b (i j)")
                 e = work.tile([P, TAPS, PAIR, PIX], F32, tag="e")
-                for b in range(PAIR):
-                    nc.gpsimd.tensor_tensor(
+                for b, engine in enumerate(engines):
+                    engine.tensor_tensor(
                         out=e[:, :, b],
                         in0=z_planes[:, :, b],
-                        in1=z_max[:, b].unsqueeze(1).to_broadcast([P, TAPS, PIX]),
+                        in1=z_max_of[c][:, b].unsqueeze(1).to_broadcast([P, TAPS, PIX]),
                         op=ALU.subtract,
                     )
-                    nc.scalar.activation(out=e[:, :, b], in_=e[:, :, b], func=ACT.Exp)
                 e_of[c] = e
 
-            def sum_e(c):
-                den_of[c] = sum_planes(e_of[c][:].rearrange("p d b (f x) -> p d (b f) x", f=2), "den_t")
+            def exponentiate(c):
+                for b in range(PAIR):
+                    nc.scalar.activation(out=e_of[c][:, :, b], in_=e_of[c][:, :, b], func=ACT.Exp)
 
-            def weigh(c):
+            def open_sum_e(c):
+                den_of[c] = banks.tile([P, BLOCKS, P], F32, name="den_t", bufs=2)
+
+            def sum_e(c, images=range(PAIR)):
+                sum_planes(den_of[c], e_of[c][:].rearrange("p d b (f x) -> p d (b f) x", f=2), images)
+
+            def weigh(c, images=slice(0, PAIR)):
                 e_maps = e_of[c][:].rearrange("p (s t) b (i j) -> p s t b i j", s=len(SHIFTS), i=SIDE)
-                times_neighbours(pv, v_of[c], lambda s, t: e_maps[:, s, t])
-                num_of[c] = sum_planes(pv_blocks, "num_t")
+                times_neighbours(pv, v_of[c], lambda s, t: e_maps[:, s, t], images)
+
+            def open_sum_pv(c):
+                num_of[c] = banks.tile([P, BLOCKS, P], F32, name="num_t", bufs=2)
+
+            def sum_pv(c, images=range(PAIR)):
+                sum_planes(num_of[c], pv_blocks, images)
 
             def reciprocal(a):
                 ln_den = work.tile([P, HALVES, BLOCKS, P], F32, tag="ln_den", bufs=1)
@@ -343,22 +361,22 @@ def tile_merge_pa_kernel(
                 nc.scalar.activation(out=r_den[:], in_=ln_den[:], func=ACT.Exp, scale=-1.0)
                 r_den_of[a] = r_den
 
-            def divide(a):
-                att = work.tile([P, HALVES, CHUNK], F32, tag="att")
-                att_sums = work.tile([P, HALVES], F32, tag="att_sums")
-                for h in range(HALVES):
-                    att_t = work.tile([P, BLOCKS, P], F32, tag="att_t")
-                    nc.vector.tensor_mul(out=att_t[:], in0=num_of[a * HALVES + h][:], in1=r_den_of[a][:, h])
-                    att_bank = banks.tile([P, BLOCKS, P], F32, tag="short")
-                    for g in range(BLOCKS):
-                        nc.tensor.transpose(att_bank[:, g, :], att_t[:, g, :], ident[:])
-                    nc.scalar.activation(
-                        out=att[:, h, :],
-                        in_=att_bank[:].rearrange("p g x -> p (g x)"),
-                        func=ACT.Copy,
-                        accum_out=att_sums[:, h : h + 1],
-                    )
-                att_of[a], sums_of[a] = att, att_sums
+            def divide(a, h):
+                att_t = work.tile([P, BLOCKS, P], F32, tag="att_t")
+                nc.vector.tensor_mul(out=att_t[:], in0=num_of[a * HALVES + h][:], in1=r_den_of[a][:, h])
+                att_bank = banks.tile([P, BLOCKS, P], F32, tag="short")
+                for g in range(BLOCKS):
+                    nc.tensor.transpose(att_bank[:, g, :], att_t[:, g, :], ident[:])
+                return att_bank[:].rearrange("p g x -> p (g x)")
+
+            def open_att(a):
+                att_of[a] = work.tile([P, HALVES, CHUNK], F32, name="att", bufs=2)
+                sums_of[a] = work.tile([P, HALVES], F32, name="att_sums", bufs=2)
+
+            def keep_att(a, h, att):
+                nc.scalar.activation(
+                    out=att_of[a][:, h, :], in_=att, func=ACT.Copy, accum_out=sums_of[a][:, h : h + 1]
+                )
 
             def statistics(a):
                 parts = work.tile([P, HALVES], F32, tag="parts")
@@ -408,51 +426,121 @@ def tile_merge_pa_kernel(
                     )
                 above_of[a], below_of[a] = above, below
 
-            def finish(a):
-                result = work.tile([P, HALVES, CHUNK], F32, tag="result")
-                for h in range(HALVES):
-                    nc.vector.scalar_tensor_tensor(
-                        out=result[:, h],
-                        in0=below_of[a][:, h],
-                        scalar=minus_slope[:],
-                        in1=above_of[a][:, h],
-                        op0=ALU.mult,
-                        op1=ALU.add,
-                    )
-                    nc.sync.dma_start(
-                        out=out_tiles[a][:, h * PAIR : (h + 1) * PAIR, :],
-                        in_=result[:, h].rearrange("p (b x) -> p b x", b=PAIR),
-                    )
+            def combine(a, h):
+                result = work.tile([P, CHUNK], F32, tag="result")
+                nc.vector.scalar_tensor_tensor(
+                    out=result[:],
+                    in0=below_of[a][:, h],
+                    scalar=minus_slope[:],
+                    in1=above_of[a][:, h],
+                    op0=ALU.mult,
+                    op1=ALU.add,
+                )
+                store(a, h, result)
+
+            def store(a, h, result):
+                nc.sync.dma_start(
+                    out=out_tiles[a][:, h * PAIR : (h + 1) * PAIR, :],
+                    in_=result[:].rearrange("p (b x) -> p b x", b=PAIR),
+                )
 
             def live(c):
                 return 0 <= c < CHUNKS
 
-            def group_due(r, lag):
-                a, rest = divmod(r - lag, HALVES)
-                return a if rest == 0 and 0 <= a < TILES else None
-
-            project_qk(0)
-            for r in range(CHUNKS + 4):
-                if live(r):
-                    products(r)
+            LAST = CHUNKS - 1
+            project_q(0)
+            project_k(0)
+            project_q(1)
+            products(0)
+            project_k(1)
+            maxima(0)
+            subtract(0, (nc.vector, nc.gpsimd))
+            exponentiate(0)
+            products(1)
+            for r in range(1, CHUNKS):
+                odd_group = (r - 3) // 2 if r % 2 == 1 and r >= 3 else None
+                even_group = (r - 2) // 2 if r % 2 == 0 else None
                 if live(r + 1):
-                    project_qk(r + 1)
-                if group_due(r, 3) is not None:
-                    divide(group_due(r, 3))
-                    statistics(group_due(r, 3))
-                if live(r - 1):
-                    sum_e(r - 1)
-                if group_due(r, 4) is not None:
-                    affine(group_due(r, 4))
-                if group_due(r, 2) is not None:
-                    reciprocal(group_due(r, 2))
-                if group_due(r, 5) is not None:
-                    finish(group_due(r, 5))
-                if live(r):
-                    stabilise(r)
-                if live(r - 1):
-                    weigh(r - 1)
-                if live(r):
-                    project_v(r)
-                if group_due(r, 3) is not None:
-                    rsqrt(group_due(r, 3))
+                    project_k(r + 1)
+                    project_q(r + 1)
+                project_v(r - 1)
+                open_sum_e(r - 1)
+                sum_e(r - 1)
+                if even_group is not None:
+                    reciprocal(even_group)
+                if odd_group is not None:
+                    statistics(odd_group)
+                    rsqrt(odd_group)
+                maxima(r)
+                subtract(r, (nc.gpsimd, nc.gpsimd))
+                if odd_group is not None:
+                    affine(odd_group)
+                exponentiate(r)
+                weigh(r - 1)
+                open_sum_pv(r - 1)
+                sum_pv(r - 1)
+                if live(r + 1):
+                    products(r + 1)
+                if even_group is not None:
+                    open_att(even_group)
+                    for h in range(HALVES):
+                        keep_att(even_group, h, divide(even_group, h))
+                if odd_group is not None and r < LAST:
+                    for h in range(HALVES):
+                        combine(odd_group, h)
+
+            a = TILES - 1
+            project_v(LAST)
+            open_sum_e(LAST)
+            open_sum_pv(LAST)
+            sum_e(LAST, (0,))
+            weigh(LAST, slice(0, 1))
+            sum_pv(LAST, (0,))
+            for h in range(HALVES):
+                combine(a - 1, h)
+            sum_e(LAST, (1,))
+            weigh(LAST, slice(1, 2))
+            sum_pv(LAST, (1,))
+            reciprocal(a)
+            stats = work.tile([P, HALVES, 6], F32, bufs=1)
+            att = work.tile([P, CHUNK], F32, name="att_last", bufs=1)
+            att_banks = []
+            for h in range(HALVES):
+                att_banks.append(divide(a, h))
+                nc.vector.bn_stats(out=stats[:, h, :], in_=att_banks[h])
+            nc.scalar.copy(out=att[:], in_=att_banks[0])
+            mean_var = work.tile([P, 2], F32, bufs=1)
+            nc.vector.bn_aggr(out=mean_var[:], in_=stats[:].rearrange("p h s -> p (h s)"))
+            var_eps = work.tile([P, 1], F32, name="var_eps_last", bufs=1)
+            nc.vector.tensor_scalar_add(out=var_eps[:], in0=mean_var[:, 1:2], scalar1=BN_EPS)
+            var_of[a] = var_eps
+            rsqrt(a)
+            gain = work.tile([P, 2], F32, name="gain_last", bufs=1)
+            nc.vector.tensor_scalar_mul(out=gain[:], in0=gamma_pm[:, a, :], scalar1=r_std_of[a][:])
+            shift = work.tile([P, 2], F32, name="shift_last", bufs=1)
+            for sign in range(2):
+                nc.vector.scalar_tensor_tensor(
+                    out=shift[:, sign : sign + 1],
+                    in0=mean_var[:, 0:1],
+                    scalar=gain[:, 1 - sign : 2 - sign],
+                    in1=beta_pm[:, a, sign : sign + 1],
+                    op0=ALU.mult,
+                    op1=ALU.add,
+                )
+            above = work.tile([P, HALVES, CHUNK], F32, tag="above")
+            below = work.tile([P, HALVES, CHUNK], F32, tag="below")
+            nc.scalar.activation(out=above[:, 0], in_=att[:], func=ACT.Relu, scale=gain[:, 0:1], bias=shift[:, 0:1])
+            nc.scalar.activation(out=below[:, 0], in_=att[:], func=ACT.Relu, scale=gain[:, 1:2], bias=shift[:, 1:2])
+            above_of[a], below_of[a] = above, below
+            n = work.tile([P, CHUNK], F32, name="n_last", bufs=1)
+            nc.vector.tensor_scalar(
+                out=n[:], in0=att_banks[1], scalar1=gain[:, 0:1], scalar2=shift[:, 0:1], op0=ALU.mult, op1=ALU.add
+            )
+            n_below = work.tile([P, CHUNK], F32, name="n_below", bufs=1)
+            nc.vector.tensor_scalar(
+                out=n_below[:], in0=n[:], scalar1=0.0, scalar2=slope_less_one[:], op0=ALU.min, op1=ALU.mult
+            )
+            result = work.tile([P, CHUNK], F32, tag="result")
+            nc.vector.tensor_tensor(out=result[:], in0=n[:], in1=n_below[:], op=ALU.add)
+            store(a, 1, result)
+            combine(a, 0)

@@ -291,8 +291,11 @@ def tile_merge_pa_kernel(
                             op=ALU.mult,
                         )
 
-            def sum_planes(total, blocks, images=range(PAIR)):
+            def sum_planes(total, blocks, images, projections):
                 for g in range(BLOCKS):
+                    if g == 1:
+                        for projection, c in projections:
+                            projection(c)
                     if g // (BLOCKS // PAIR) in images:
                         for d in range(TAPS):
                             nc.tensor.matmul(
@@ -340,8 +343,9 @@ def tile_merge_pa_kernel(
             def open_sum_e(c):
                 den_of[c] = banks.tile([P, BLOCKS, P], F32, name="den_t", bufs=2)
 
-            def sum_e(c, images=range(PAIR)):
-                sum_planes(den_of[c], e_of[c][:].rearrange("p d b (f x) -> p d (b f) x", f=2), images)
+            def sum_e(c, images=range(PAIR), projections=()):
+                blocks = e_of[c][:].rearrange("p d b (f x) -> p d (b f) x", f=2)
+                sum_planes(den_of[c], blocks, images, projections)
 
             def weigh(c, images=slice(0, PAIR)):
                 e_maps = e_of[c][:].rearrange("p (s t) b (i j) -> p s t b i j", s=len(SHIFTS), i=SIDE)
@@ -350,8 +354,8 @@ def tile_merge_pa_kernel(
             def open_sum_pv(c):
                 num_of[c] = banks.tile([P, BLOCKS, P], F32, name="num_t", bufs=2)
 
-            def sum_pv(c, images=range(PAIR)):
-                sum_planes(num_of[c], pv_blocks, images)
+            def sum_pv(c, images=range(PAIR), projections=()):
+                sum_planes(num_of[c], pv_blocks, images, projections)
 
             def reciprocal(a):
                 ln_den = work.tile([P, HALVES, BLOCKS, P], F32, tag="ln_den", bufs=1)
@@ -453,6 +457,7 @@ def tile_merge_pa_kernel(
             project_q(1)
             products(0)
             project_k(1)
+            project_v(0)
             maxima(0)
             subtract(0, (nc.vector, nc.gpsimd))
             exponentiate(0)
@@ -460,12 +465,8 @@ def tile_merge_pa_kernel(
             for r in range(1, CHUNKS):
                 odd_group = (r - 3) // 2 if r % 2 == 1 and r >= 3 else None
                 even_group = (r - 2) // 2 if r % 2 == 0 else None
-                if live(r + 1):
-                    project_k(r + 1)
-                    project_q(r + 1)
-                project_v(r - 1)
                 open_sum_e(r - 1)
-                sum_e(r - 1)
+                sum_e(r - 1, projections=((project_k, r + 1), (project_q, r + 1)) if live(r + 1) else ())
                 if even_group is not None:
                     reciprocal(even_group)
                 if odd_group is not None:
@@ -478,7 +479,7 @@ def tile_merge_pa_kernel(
                 exponentiate(r)
                 weigh(r - 1)
                 open_sum_pv(r - 1)
-                sum_pv(r - 1)
+                sum_pv(r - 1, projections=((project_v, r),))
                 if live(r + 1):
                     products(r + 1)
                 if even_group is not None:
@@ -490,7 +491,6 @@ def tile_merge_pa_kernel(
                         combine(odd_group, h)
 
             a = TILES - 1
-            project_v(LAST)
             open_sum_e(LAST)
             open_sum_pv(LAST)
             sum_e(LAST, (0,))

@@ -55,12 +55,16 @@ def tile_merge_pa_kernel(
         z_even = keep.tile([P, len(SHIFTS), len(SHIFTS), PAIR, SIDE, SIDE], F32)
         z_odd = keep.tile([P, len(SHIFTS), len(SHIFTS), PAIR, SIDE, SIDE], F32)
         pv = keep.tile([P, len(SHIFTS), len(SHIFTS), PAIR, SIDE, SIDE], F32)
-        nc.gpsimd.memset(pv[:], 0.0)
-        for planes in (z_even, z_odd):
-            nc.vector.memset(planes[:, 0, :, :, 0, :], 0.0)
-            nc.vector.memset(planes[:, 2, :, :, SIDE - 1, :], 0.0)
-            nc.vector.memset(planes[:, :, 0, :, :, 0], 0.0)
-            nc.vector.memset(planes[:, :, 2, :, :, SIDE - 1], 0.0)
+        zeros = keep.tile([P, len(SHIFTS), PAIR, SIDE], F32)
+        nc.vector.memset(zeros[:], 0.0)
+
+        def zero_borders(planes, zero):
+            zero(planes[:, 0, :, :, 0, :])
+            zero(planes[:, 2, :, :, SIDE - 1, :])
+            zero(planes[:, :, 0, :, :, 0])
+            zero(planes[:, :, 2, :, :, SIDE - 1])
+
+        zero_borders(z_even, lambda border: nc.vector.memset(border, 0.0))
 
         bias_c1 = keep.tile([P, PACK], F32)
         gamma_pm = keep.tile([P, TILES, 2], F32)
@@ -224,6 +228,9 @@ def tile_merge_pa_kernel(
                     add_bias(2 * b - 3)
                 add_columns(b, 1)
                 turn_weight(name)
+                if b == 0:
+                    for planes in (z_odd, pv):
+                        zero_borders(planes, lambda border: nc.scalar.copy(out=border, in_=zeros[:]))
             quantise_weight("q")
             quantise_ll(3)
             multiply_y(6)
@@ -324,21 +331,19 @@ def tile_merge_pa_kernel(
                     nc.vector.tensor_max(out=z_max[:, b], in0=top[:, 0, b], in1=z_planes[:, 8, b])
                 z_max_of[c] = z_max
 
-            def subtract(c, engines):
-                z_planes = z_pair[c % 2][:].rearrange("p s t b i j -> p (s t) b (i j)")
-                e = work.tile([P, TAPS, PAIR, PIX], F32, tag="e")
-                for b, engine in enumerate(engines):
-                    engine.tensor_tensor(
-                        out=e[:, :, b],
-                        in0=z_planes[:, :, b],
-                        in1=z_max_of[c][:, b].unsqueeze(1).to_broadcast([P, TAPS, PIX]),
-                        op=ALU.subtract,
-                    )
-                e_of[c] = e
+            def open_e(c):
+                e_of[c] = work.tile([P, TAPS, PAIR, PIX], F32, name="e", bufs=2)
 
-            def exponentiate(c):
-                for b in range(PAIR):
-                    nc.scalar.activation(out=e_of[c][:, :, b], in_=e_of[c][:, :, b], func=ACT.Exp)
+            def subtract(c, b, engine):
+                engine.tensor_tensor(
+                    out=e_of[c][:, :, b],
+                    in0=z_pair[c % 2][:].rearrange("p s t b i j -> p (s t) b (i j)")[:, :, b],
+                    in1=z_max_of[c][:, b].unsqueeze(1).to_broadcast([P, TAPS, PIX]),
+                    op=ALU.subtract,
+                )
+
+            def exponentiate(c, b):
+                nc.scalar.activation(out=e_of[c][:, :, b], in_=e_of[c][:, :, b], func=ACT.Exp)
 
             def open_sum_e(c):
                 den_of[c] = banks.tile([P, BLOCKS, P], F32, name="den_t", bufs=2)
@@ -459,36 +464,41 @@ def tile_merge_pa_kernel(
             project_k(1)
             project_v(0)
             maxima(0)
-            subtract(0, (nc.vector, nc.gpsimd))
-            exponentiate(0)
+            open_e(0)
+            for b, engine in enumerate((nc.vector, nc.gpsimd)):
+                subtract(0, b, engine)
+                exponentiate(0, b)
             products(1)
             for r in range(1, CHUNKS):
-                odd_group = (r - 3) // 2 if r % 2 == 1 and r >= 3 else None
-                even_group = (r - 2) // 2 if r % 2 == 0 else None
+                a = r // 2 - 1
+                even = r % 2 == 0
                 open_sum_e(r - 1)
                 sum_e(r - 1, projections=((project_k, r + 1), (project_q, r + 1)) if live(r + 1) else ())
-                if even_group is not None:
-                    reciprocal(even_group)
-                if odd_group is not None:
-                    statistics(odd_group)
-                    rsqrt(odd_group)
+                if even:
+                    reciprocal(a)
+                elif a >= 0:
+                    statistics(a)
                 maxima(r)
-                subtract(r, (nc.gpsimd, nc.gpsimd))
-                if odd_group is not None:
-                    affine(odd_group)
-                exponentiate(r)
+                open_e(r)
+                subtract(r, 0, nc.gpsimd)
+                exponentiate(r, 0)
+                if not even and a >= 0:
+                    rsqrt(a)
+                    affine(a)
+                subtract(r, 1, nc.gpsimd)
+                exponentiate(r, 1)
                 weigh(r - 1)
                 open_sum_pv(r - 1)
                 sum_pv(r - 1, projections=((project_v, r),))
                 if live(r + 1):
                     products(r + 1)
-                if even_group is not None:
-                    open_att(even_group)
+                if even:
+                    open_att(a)
                     for h in range(HALVES):
-                        keep_att(even_group, h, divide(even_group, h))
-                if odd_group is not None and r < LAST:
+                        keep_att(a, h, divide(a, h))
+                elif a >= 0 and r < LAST:
                     for h in range(HALVES):
-                        combine(odd_group, h)
+                        combine(a, h)
 
             a = TILES - 1
             open_sum_e(LAST)

@@ -1,3 +1,5 @@
+from functools import partial
+
 import concourse.mybir as mybir
 from concourse.masks import make_identity
 
@@ -17,6 +19,7 @@ SIDE = 16
 PIX = SIDE * SIDE
 PAIR = 2
 CHUNK = PAIR * PIX
+PAD = 4
 TILES = CHANNELS // P
 HALVES = IMAGES // PAIR
 CHUNKS = TILES * HALVES
@@ -51,18 +54,28 @@ def tile_merge_pa_kernel(
             w_scales[name] = keep.tile([P, CHANNELS], U8, name="scales_" + name, align_bytes=64)
         y_codes = keep.tile([P, IMAGES * PIX], U32, align_bytes=64)
         y_scales = keep.tile([P, IMAGES * PIX], U8, align_bytes=64)
+        y_left = keep.tile([P, IMAGES * PIX], U32, align_bytes=64)
+        y_right = keep.tile([P, IMAGES * PIX], U32, align_bytes=64)
+        for words, edge in ((y_left, SIDE - 1), (y_right, 0)):
+            nc.gpsimd.memset(words[:].rearrange("p (r j) -> p r j", j=SIDE)[:, :, edge : edge + 1], 0)
 
-        z_even = keep.tile([P, len(SHIFTS), len(SHIFTS), PAIR, SIDE, SIDE], F32)
-        z_odd = keep.tile([P, len(SHIFTS), len(SHIFTS), PAIR, SIDE, SIDE], F32)
-        pv = keep.tile([P, len(SHIFTS), len(SHIFTS), PAIR, SIDE, SIDE], F32)
-        zeros = keep.tile([P, len(SHIFTS), PAIR, SIDE], F32)
+        z_even = keep.tile([P, TAPS, PAIR, PIX], F32)
+        z_odd = keep.tile([P, TAPS, PAIR, PIX], F32)
+        pv = keep.tile([P, TAPS, PAIR, PIX], F32)
+        k_pads = [keep.tile([P, PAIR * SIDE + 1, PAD + SIDE], F32, name="k_pad%d" % i) for i in range(2)]
+        zeros = keep.tile([P, PAIR * SIDE + 1, PAD], F32)
         nc.vector.memset(zeros[:], 0.0)
 
         def zero_borders(planes, zero):
-            zero(planes[:, 0, :, :, 0, :])
-            zero(planes[:, 2, :, :, SIDE - 1, :])
-            zero(planes[:, :, 0, :, :, 0])
-            zero(planes[:, :, 2, :, :, SIDE - 1])
+            zero(planes[:, 0:3, :, 0 : SIDE + 1])
+            zero(planes[:, 3:6, :, 0:1])
+            zero(planes[:, 3:6, :, PIX - 1 : PIX])
+            zero(planes[:, 6:9, :, PIX - SIDE - 1 : PIX])
+
+        def copy_zeros(border):
+            dims = border.shape
+            source = zeros[:].rearrange("p r w -> p (r w)")[:, 0 : dims[1] * dims[2] * dims[3]]
+            nc.scalar.copy(out=border, in_=source.rearrange("p (a b c) -> p a b c", a=dims[1], b=dims[2]))
 
         zero_borders(z_even, lambda border: nc.vector.memset(border, 0.0))
 
@@ -209,6 +222,11 @@ def tile_merge_pa_kernel(
                     scales=y_scales[:, cols],
                     in_=y_bf[:, cols, :].rearrange("p x t -> p (x t)"),
                 )
+                whole = y_codes[:, cols].rearrange("p (r j) -> p r j", j=SIDE)
+                for words, kept in ((y_left, slice(0, SIDE - 1)), (y_right, slice(1, SIDE))):
+                    nc.gpsimd.tensor_copy(
+                        out=words[:, cols].rearrange("p (r j) -> p r j", j=SIDE)[:, :, kept], in_=whole[:, :, kept]
+                    )
 
             for b, name in enumerate(("c1", "q", "k", "v")):
                 add_rows(b, 0)
@@ -229,8 +247,10 @@ def tile_merge_pa_kernel(
                 add_columns(b, 1)
                 turn_weight(name)
                 if b == 0:
+                    for k_pad in k_pads:
+                        nc.scalar.copy(out=k_pad[:, :, 0:PAD], in_=zeros[:])
                     for planes in (z_odd, pv):
-                        zero_borders(planes, lambda border: nc.scalar.copy(out=border, in_=zeros[:]))
+                        zero_borders(planes, copy_zeros)
             quantise_weight("q")
             quantise_ll(3)
             multiply_y(6)
@@ -251,58 +271,45 @@ def tile_merge_pa_kernel(
             nc.scalar.add(out=slope_less_one[:], in_=slope_bf[:], add=-1.0)
 
         z_pair = (z_even, z_odd)
-        pv_blocks = pv[:].rearrange("p s t b (f i) j -> p (s t) (b f) (i j)", f=2)
         out_tiles = out.rearrange("b (r a) h w -> a r b (h w)", a=TILES)
-        q_of, k_of, v_of, z_max_of, e_of, den_of, num_of = {}, {}, {}, {}, {}, {}, {}
+        q_of, v_of, z_max_of, e_of, den_of, num_of = {}, {}, {}, {}, {}, {}
         r_den_of, att_of, sums_of, mean_of, var_of, r_std_of, above_of, below_of = {}, {}, {}, {}, {}, {}, {}, {}
 
         with tc.tile_pool(name="work", bufs=2) as work, tc.psum_pool(name="banks", bufs=2) as banks:
 
-            def project(name, c, tag, bufs):
+            def project(name, codes, c, tag, bufs):
                 a, h = divmod(c, HALVES)
-                bank = banks.tile([P, PAIR, SIDE, SIDE], F32, tag=tag, bufs=bufs)
+                bank = banks.tile([P, CHUNK], F32, tag=tag, bufs=bufs)
                 rows = slice(a * P, (a + 1) * P)
                 cols = slice(h * CHUNK, (h + 1) * CHUNK)
                 nc.tensor.matmul_mx(
-                    out=bank[:].rearrange("p b i j -> p (b i j)"),
+                    out=bank[:],
                     lhsT=w_codes[name][:, rows].bitcast(FP8X4),
                     lhsT_scale=w_scales[name][:, rows],
-                    rhs=y_codes[:, cols].bitcast(FP8X4),
+                    rhs=codes[:, cols].bitcast(FP8X4),
                     rhs_scale=y_scales[:, cols],
                     start=True,
                     stop=True,
                 )
                 return bank
 
-            def project_k(c):
-                k_of[c] = project("k", c, "bank_k", 1)
-
             def project_q(c):
-                q_bank = project("q", c, "short", 2)
-                q_sb = work.tile([P, PAIR, SIDE, SIDE], F32, tag="q_sb")
-                nc.scalar.copy(out=q_sb[:], in_=q_bank[:])
-                q_of[c] = q_sb
+                q_of[c] = project("q", y_codes, c, "bank_q", 1)
 
-            def project_v(c):
-                v_of[c] = project("v", c, "bank_v", 1)
+            def project_k(c):
+                k_bank = project("k", y_codes, c, "bank_k", 1)
+                nc.scalar.copy(
+                    out=k_pads[c % 2][:, 0 : PAIR * SIDE, PAD:], in_=k_bank[:].rearrange("p (r j) -> p r j", j=SIDE)
+                )
 
-            def times_neighbours(planes, bank, maps, images=slice(0, PAIR)):
-                for s, di in enumerate(SHIFTS):
-                    i0, i1 = inside(di)
-                    for t, dj in enumerate(SHIFTS):
-                        j0, j1 = inside(dj)
-                        nc.vector.tensor_tensor(
-                            out=planes[:, s, t, images, i0:i1, j0:j1],
-                            in0=bank[:, images, i0 + di : i1 + di, j0 + dj : j1 + dj],
-                            in1=maps(s, t)[:, images, i0:i1, j0:j1],
-                            op=ALU.mult,
-                        )
+            def project_v(c, t, tag="bank_v", bufs=2):
+                v_of[c, t] = project("v", (y_left, y_codes, y_right)[t], c, tag, bufs)
 
             def sum_planes(total, blocks, images, projections):
                 for g in range(BLOCKS):
                     if g == 1:
-                        for projection, c in projections:
-                            projection(c)
+                        for projection in projections:
+                            projection()
                     if g // (BLOCKS // PAIR) in images:
                         for d in range(TAPS):
                             nc.tensor.matmul(
@@ -315,10 +322,24 @@ def tile_merge_pa_kernel(
                             )
 
             def products(c):
-                times_neighbours(z_pair[c % 2], k_of[c], lambda s, t: q_of[c])
+                k_flat = k_pads[c % 2][:].rearrange("p r w -> p (r w)")
+                width = PAD + SIDE
+                for s, di in enumerate(SHIFTS):
+                    i0, i1 = inside(di)
+                    for t, dj in enumerate(SHIFTS):
+                        k_rows = k_flat[:, PAD + dj : PAD + dj + PAIR * SIDE * width].rearrange(
+                            "p (b i w) -> p b i w", b=PAIR, w=width
+                        )
+                        z = z_pair[c % 2][:, s * 3 + t].rearrange("p b (i j) -> p b i j", j=SIDE)
+                        nc.vector.tensor_tensor(
+                            out=z[:, :, i0:i1],
+                            in0=q_of[c][:].rearrange("p (b i j) -> p b i j", b=PAIR, j=SIDE)[:, :, i0:i1],
+                            in1=k_rows[:, :, i0 + di : i1 + di, 0:SIDE],
+                            op=ALU.mult,
+                        )
 
             def maxima(c):
-                z_planes = z_pair[c % 2][:].rearrange("p s t b i j -> p (s t) b (i j)")
+                z_planes = z_pair[c % 2]
                 top = work.tile([P, 4, PAIR, PIX], F32, tag="top")
                 z_max = work.tile([P, PAIR, PIX], F32, tag="z_max")
                 for b in range(PAIR):
@@ -337,7 +358,7 @@ def tile_merge_pa_kernel(
             def subtract(c, b, engine):
                 engine.tensor_tensor(
                     out=e_of[c][:, :, b],
-                    in0=z_pair[c % 2][:].rearrange("p s t b i j -> p (s t) b (i j)")[:, :, b],
+                    in0=z_pair[c % 2][:, :, b],
                     in1=z_max_of[c][:, b].unsqueeze(1).to_broadcast([P, TAPS, PIX]),
                     op=ALU.subtract,
                 )
@@ -352,15 +373,30 @@ def tile_merge_pa_kernel(
                 blocks = e_of[c][:].rearrange("p d b (f x) -> p d (b f) x", f=2)
                 sum_planes(den_of[c], blocks, images, projections)
 
-            def weigh(c, images=slice(0, PAIR)):
-                e_maps = e_of[c][:].rearrange("p (s t) b (i j) -> p s t b i j", s=len(SHIFTS), i=SIDE)
-                times_neighbours(pv, v_of[c], lambda s, t: e_maps[:, s, t], images)
+            def weigh(c, t, planes, images=slice(0, PAIR)):
+                v_maps = v_of[c, t][:].rearrange("p (b x) -> p b x", b=PAIR)
+                for s, di in enumerate(SHIFTS):
+                    i0, i1 = inside(di)
+                    shift = SIDE * di + SHIFTS[t]
+                    first = max(SIDE * i0, -shift)
+                    last = min(SIDE * i1, PIX - shift)
+                    nc.vector.tensor_tensor(
+                        out=planes[:, s * 3 + t, images, first:last],
+                        in0=v_maps[:, images, first + shift : last + shift],
+                        in1=e_of[c][:, s * 3 + t, images, first:last],
+                        op=ALU.mult,
+                    )
+
+            def pixel_bank():
+                bank = banks.tile([P, BLOCKS, P], F32, tag="num_t", bufs=2)
+                return bank
 
             def open_sum_pv(c):
-                num_of[c] = banks.tile([P, BLOCKS, P], F32, name="num_t", bufs=2)
+                num_of[c] = pixel_bank()
 
-            def sum_pv(c, images=range(PAIR), projections=()):
-                sum_planes(num_of[c], pv_blocks, images, projections)
+            def sum_pv(c, planes, images=range(PAIR), projections=()):
+                blocks = planes[:].rearrange("p d b (f x) -> p d (b f) x", f=2)
+                sum_planes(num_of[c], blocks, images, projections)
 
             def reciprocal(a):
                 ln_den = work.tile([P, HALVES, BLOCKS, P], F32, tag="ln_den", bufs=1)
@@ -373,7 +409,7 @@ def tile_merge_pa_kernel(
             def divide(a, h):
                 att_t = work.tile([P, BLOCKS, P], F32, tag="att_t")
                 nc.vector.tensor_mul(out=att_t[:], in0=num_of[a * HALVES + h][:], in1=r_den_of[a][:, h])
-                att_bank = banks.tile([P, BLOCKS, P], F32, tag="short")
+                att_bank = pixel_bank()
                 for g in range(BLOCKS):
                     nc.tensor.transpose(att_bank[:, g, :], att_t[:, g, :], ident[:])
                 return att_bank[:].rearrange("p g x -> p (g x)")
@@ -457,12 +493,13 @@ def tile_merge_pa_kernel(
                 return 0 <= c < CHUNKS
 
             LAST = CHUNKS - 1
-            project_q(0)
             project_k(0)
-            project_q(1)
-            products(0)
+            project_q(0)
             project_k(1)
-            project_v(0)
+            products(0)
+            project_q(1)
+            project_v(0, 0)
+            project_v(0, 1)
             maxima(0)
             open_e(0)
             for b, engine in enumerate((nc.vector, nc.gpsimd)):
@@ -473,23 +510,29 @@ def tile_merge_pa_kernel(
                 a = r // 2 - 1
                 even = r % 2 == 0
                 open_sum_e(r - 1)
-                sum_e(r - 1, projections=((project_k, r + 1), (project_q, r + 1)) if live(r + 1) else ())
+                sum_e(
+                    r - 1,
+                    projections=(partial(project_k, r + 1), partial(project_q, r + 1)) if live(r + 1) else (),
+                )
                 if even:
                     reciprocal(a)
                 elif a >= 0:
                     statistics(a)
                 maxima(r)
                 open_e(r)
-                subtract(r, 0, nc.gpsimd)
+                subtract(r, 0, nc.gpsimd if r < LAST else nc.vector)
                 exponentiate(r, 0)
                 if not even and a >= 0:
                     rsqrt(a)
                     affine(a)
                 subtract(r, 1, nc.gpsimd)
                 exponentiate(r, 1)
-                weigh(r - 1)
+                weigh(r - 1, 0, pv)
+                project_v(r - 1, 2)
+                weigh(r - 1, 1, pv)
+                weigh(r - 1, 2, pv)
                 open_sum_pv(r - 1)
-                sum_pv(r - 1, projections=((project_v, r),))
+                sum_pv(r - 1, pv, projections=(partial(project_v, r, 0), partial(project_v, r, 1)))
                 if live(r + 1):
                     products(r + 1)
                 if even:
@@ -503,20 +546,21 @@ def tile_merge_pa_kernel(
             a = TILES - 1
             open_sum_e(LAST)
             open_sum_pv(LAST)
-            sum_e(LAST, (0,))
-            weigh(LAST, slice(0, 1))
-            sum_pv(LAST, (0,))
+            pv_last = z_pair[(LAST - 1) % 2]
+            project_v(LAST, 2, "bank_q", 1)
+            for b in range(PAIR):
+                sum_e(LAST, (b,))
+            for b in range(2):
+                for t in range(len(SHIFTS)):
+                    weigh(LAST, t, pv_last, slice(b, b + 1))
+                sum_pv(LAST, pv_last, (b,))
             for h in range(HALVES):
                 combine(a - 1, h)
-            sum_e(LAST, (1,))
-            weigh(LAST, slice(1, 2))
-            sum_pv(LAST, (1,))
             reciprocal(a)
             stats = work.tile([P, HALVES, 6], F32, bufs=1)
             att = work.tile([P, CHUNK], F32, name="att_last", bufs=1)
-            att_banks = []
+            att_banks = [divide(a, h) for h in range(HALVES)]
             for h in range(HALVES):
-                att_banks.append(divide(a, h))
                 nc.vector.bn_stats(out=stats[:, h, :], in_=att_banks[h])
             nc.scalar.copy(out=att[:], in_=att_banks[0])
             mean_var = work.tile([P, 2], F32, bufs=1)

@@ -43,9 +43,11 @@ def tile_merge_pa_kernel(
     nc = tc.nc
     weights = {"c1": w_c1, "q": w_q, "k": w_k, "v": w_v}
 
-    with tc.tile_pool(name="keep", bufs=1) as keep, tc.manual_schedule():
+    with tc.tile_pool(name="keep", bufs=1) as keep, tc.psum_pool(name="banks", bufs=2) as banks, tc.manual_schedule():
         ident = keep.tile([P, P], F32)
         make_identity(nc, ident[:])
+        ident_bf = keep.tile([P, P], BF16)
+        make_identity(nc, ident_bf[:])
 
         w_codes = {}
         w_scales = {}
@@ -89,7 +91,87 @@ def tile_merge_pa_kernel(
         eps = keep.tile([P, 1], F32)
         nc.gpsimd.memset(eps[:], BN_EPS)
 
-        with tc.tile_pool(name="head", bufs=2) as head, tc.psum_pool(name="head_banks", bufs=4) as head_banks:
+        z_pair = (z_even, z_odd)
+        q_of, v_of, z_max_of, e_of, den_of, num_of = {}, {}, {}, {}, {}, {}
+
+        def project(name, codes, c, tag, bufs):
+            a, h = divmod(c, HALVES)
+            bank = banks.tile([P, CHUNK], F32, tag=tag, bufs=bufs)
+            rows = slice(a * P, (a + 1) * P)
+            cols = slice(h * CHUNK, (h + 1) * CHUNK)
+            nc.tensor.matmul_mx(
+                out=bank[:],
+                lhsT=w_codes[name][:, rows].bitcast(FP8X4),
+                lhsT_scale=w_scales[name][:, rows],
+                rhs=codes[:, cols].bitcast(FP8X4),
+                rhs_scale=y_scales[:, cols],
+                start=True,
+                stop=True,
+            )
+            return bank
+
+        def project_q(c):
+            q_of[c] = project("q", y_codes, c, "bank_q", 1)
+
+        def project_k(c):
+            k_bank = project("k", y_codes, c, "bank_k", 1)
+            nc.scalar.copy(
+                out=k_pads[c % 2][:, 0 : PAIR * SIDE, PAD:], in_=k_bank[:].rearrange("p (r j) -> p r j", j=SIDE)
+            )
+
+        def project_v(c, t, tag="bank_v", bufs=2):
+            v_of[c, t] = project("v", (y_left, y_codes, y_right)[t], c, tag, bufs)
+
+        def products(c):
+            k_flat = k_pads[c % 2][:].rearrange("p r w -> p (r w)")
+            width = PAD + SIDE
+            for s, di in enumerate(SHIFTS):
+                i0, i1 = inside(di)
+                for t, dj in enumerate(SHIFTS):
+                    k_rows = k_flat[:, PAD + dj : PAD + dj + PAIR * SIDE * width].rearrange(
+                        "p (b i w) -> p b i w", b=PAIR, w=width
+                    )
+                    z = z_pair[c % 2][:, s * 3 + t].rearrange("p b (i j) -> p b i j", j=SIDE)
+                    nc.vector.tensor_tensor(
+                        out=z[:, :, i0:i1],
+                        in0=q_of[c][:].rearrange("p (b i j) -> p b i j", b=PAIR, j=SIDE)[:, :, i0:i1],
+                        in1=k_rows[:, :, i0 + di : i1 + di, 0:SIDE],
+                        op=ALU.mult,
+                    )
+
+        def maxima(c, before_last=()):
+            z_planes = z_pair[c % 2]
+            top = keep.tile([P, 4, PAIR, PIX], F32, tag="top")
+            z_max = keep.tile([P, PAIR, PIX], F32, tag="z_max", bufs=2)
+            for b in range(PAIR):
+                nc.vector.tensor_max(out=top[:, :, b], in0=z_planes[:, 0:4, b], in1=z_planes[:, 4:8, b])
+            for b in range(PAIR):
+                nc.vector.tensor_max(out=top[:, 0:2, b], in0=top[:, 0:2, b], in1=top[:, 2:4, b])
+            for b in range(PAIR):
+                nc.vector.tensor_max(out=top[:, 0, b], in0=top[:, 0, b], in1=top[:, 1, b])
+            for b in range(PAIR):
+                if b == PAIR - 1:
+                    for step in before_last:
+                        step()
+                nc.vector.tensor_max(out=z_max[:, b], in0=top[:, 0, b], in1=z_planes[:, 8, b])
+            z_max_of[c] = z_max
+
+        def open_e(c):
+            e = keep.tile([P, TAPS, PAIR, PIX], F32, tag="e", bufs=2)
+            e_of[c] = e
+
+        def subtract(c, b, engine):
+            engine.tensor_tensor(
+                out=e_of[c][:, :, b],
+                in0=z_pair[c % 2][:, :, b],
+                in1=z_max_of[c][:, b].unsqueeze(1).to_broadcast([P, TAPS, PIX]),
+                op=ALU.subtract,
+            )
+
+        def exponentiate(c, b):
+            nc.scalar.activation(out=e_of[c][:, :, b], in_=e_of[c][:, :, b], func=ACT.Exp)
+
+        with tc.tile_pool(name="head", bufs=2) as head:
             x_sb = []
             w_raw = {}
 
@@ -111,10 +193,11 @@ def tile_merge_pa_kernel(
             load_image(1, 1)
             b1_bf = head.tile([P, PACK], BF16, bufs=1)
             nc.sync.dma_start(out=b1_bf[:], in_=b_c1.rearrange("(r t) -> r t", t=PACK))
+            load_weight("q")
+            load_weight("k")
             load_image(2, 1)
             load_image(3, 1)
-            for name in ("q", "k", "v"):
-                load_weight(name)
+            load_weight("v")
             gamma_bf = head.tile([P, TILES], BF16, bufs=1)
             nc.sync.dma_start(out=gamma_bf[:], in_=bn_gamma.rearrange("(r a) -> r a", a=TILES))
             beta_bf = head.tile([P, TILES], BF16, bufs=1)
@@ -129,7 +212,7 @@ def tile_merge_pa_kernel(
                 grouped = head.tile([P, TILES * P * PACK], BF16, name="grouped_" + name, bufs=1, align_bytes=64)
                 grouped_words = grouped[:].bitcast(F32).rearrange("p (a r u) -> p a r u", a=TILES, u=2)
                 for first in range(0, TILES, 2):
-                    turned = head_banks.tile([P, 2, 2, P], F32, tag="turned")
+                    turned = banks.tile([P, 2, 2, P], F32, tag="den_t", bufs=2)
                     for a in range(2):
                         for u in range(2):
                             row = (first + a) * 2 * P
@@ -151,31 +234,44 @@ def tile_merge_pa_kernel(
             ll_scales = head.tile([P, IMAGES * PIX], U8, bufs=1, align_bytes=64)
             row_sums_of, ll2_of = {}, {}
 
-            def add_rows(b, part):
-                if part == 0:
-                    row_sums_of[b] = head.tile([P, PACK * PIX * 2], F32, name="row_sums", bufs=2)
-                half = PACK * PIX
-                row_pairs = x_sb[b][:, 2 * part * half : 2 * (part + 1) * half].rearrange(
-                    "p (r two w) -> p r two w", two=2, w=2 * SIDE
-                )
+            def open_ll(b):
+                row_sums_of[b] = head.tile([P, PACK, SIDE, 2 * SIDE], F32, name="row_sums", bufs=2)
+                ll2_of[b] = head.tile([P, PIX, PACK], BF16, name="ll2", bufs=2, align_bytes=64)
+
+            def add_rows(b, channels=slice(0, PACK), rows=slice(0, SIDE)):
+                x_rows = x_sb[b][:].rearrange("p (t i two w) -> p t i two w", t=PACK, i=SIDE, two=2)
                 nc.vector.tensor_tensor(
-                    out=row_sums_of[b][:, part * half : (part + 1) * half].rearrange("p (r w) -> p r w", w=2 * SIDE),
-                    in0=row_pairs[:, :, 0, :],
-                    in1=row_pairs[:, :, 1, :],
+                    out=row_sums_of[b][:, channels, rows],
+                    in0=x_rows[:, channels, rows, 0, :],
+                    in1=x_rows[:, channels, rows, 1, :],
                     op=ALU.add,
                 )
 
             def add_columns(b, part):
-                if part == 0:
-                    ll2_of[b] = head.tile([P, PIX, PACK], BF16, name="ll2", bufs=2, align_bytes=64)
-                pixels = slice(part * PIX // 2, (part + 1) * PIX // 2)
-                col_pairs = row_sums_of[b][:].rearrange("p (t x two) -> p t x two", t=PACK, two=2)[:, :, pixels, :]
+                pixels = slice(part * P, (part + 1) * P)
+                col_pairs = row_sums_of[b][:].rearrange("p t i (j two) -> p t (i j) two", two=2)[:, :, pixels, :]
                 col_pairs = col_pairs.rearrange("p t (c i) two -> p c t i two", i=RUN)
                 nc.vector.tensor_tensor(
                     out=ll2_of[b][:, pixels, :].rearrange("p (c i) t -> p c t i", i=RUN),
                     in0=col_pairs[:, :, :, :, 0],
                     in1=col_pairs[:, :, :, :, 1],
                     op=ALU.add,
+                )
+
+            def sum_squares_on_tensor(b, part):
+                rows = slice(part * P // SIDE, (part + 1) * P // SIDE)
+                squares = x_sb[b][:].rearrange("p (t i a j c) -> p t i a j c", t=PACK, i=SIDE, a=2, j=SIDE)
+                ll_bank = banks.tile([P, PACK, P], F32, tag="bank_v", bufs=2)
+                for n in range(4):
+                    nc.tensor.matmul(
+                        out=ll_bank[:].rearrange("p t (i j) -> p t i j", j=SIDE),
+                        lhsT=ident_bf[:],
+                        rhs=squares[:, :, rows, n // 2, :, n % 2],
+                        start=(n == 0),
+                        stop=(n == 3),
+                    )
+                nc.scalar.copy(
+                    out=ll2_of[b][:, part * P : (part + 1) * P, :], in_=ll_bank[:].rearrange("p t x -> p x t")
                 )
 
             def quantise_ll(b):
@@ -191,7 +287,7 @@ def tile_merge_pa_kernel(
 
             def multiply_y(g):
                 cols = slice(g * P, (g + 1) * P)
-                y_bank = head_banks.tile([P, PACK, P], F32, tag="y_bank")
+                y_bank = banks.tile([P, PACK, P], F32, tag="num_t", bufs=2)
                 for t in range(PACK):
                     rows = slice(t * P, (t + 1) * P)
                     nc.tensor.matmul_mx(
@@ -215,6 +311,16 @@ def tile_merge_pa_kernel(
                     op1=ALU.add,
                 )
 
+            def add_bias_on_scalar(g):
+                for t in range(PACK):
+                    nc.scalar.activation(
+                        out=y_bf[:, g * P : (g + 1) * P, t],
+                        in_=y_bank_of[g][:, t, :],
+                        func=ACT.Identity,
+                        scale=0.5,
+                        bias=bias_c1[:, t : t + 1],
+                    )
+
             def quantise_y(h):
                 cols = slice(h * CHUNK, (h + 1) * CHUNK)
                 nc.vector.quantize_mx(
@@ -228,41 +334,67 @@ def tile_merge_pa_kernel(
                         out=words[:, cols].rearrange("p (r j) -> p r j", j=SIDE)[:, :, kept], in_=whole[:, :, kept]
                     )
 
-            for b, name in enumerate(("c1", "q", "k", "v")):
-                add_rows(b, 0)
-                if b >= 1:
-                    quantise_ll(b - 1)
-                add_rows(b, 1)
+            turn_weight("c1")
+            for k_pad in k_pads:
+                nc.scalar.copy(out=k_pad[:, :, 0:PAD], in_=zeros[:])
+            for planes in (z_odd, pv):
+                zero_borders(planes, copy_zeros)
+            nc.scalar.copy(out=bias_c1[:], in_=b1_bf[:])
+            for b in range(2):
+                open_ll(b)
+                add_rows(b, channels=slice(0, 2))
+                if b == 1:
+                    quantise_ll(0)
+                add_rows(b, channels=slice(2, 4))
                 if b == 1:
                     quantise_weight("c1")
-                    nc.scalar.copy(out=bias_c1[:], in_=b1_bf[:])
-                if b >= 1:
-                    multiply_y(2 * b - 2)
-                    multiply_y(2 * b - 1)
-                if b >= 2:
-                    add_bias(2 * b - 4)
+                    turn_weight("q")
+                    multiply_y(0)
+                    multiply_y(1)
+                    turn_weight("k")
                 add_columns(b, 0)
-                if b >= 2:
-                    add_bias(2 * b - 3)
                 add_columns(b, 1)
-                turn_weight(name)
-                if b == 0:
-                    for k_pad in k_pads:
-                        nc.scalar.copy(out=k_pad[:, :, 0:PAD], in_=zeros[:])
-                    for planes in (z_odd, pv):
-                        zero_borders(planes, copy_zeros)
+            add_bias(0)
+            quantise_ll(1)
+            multiply_y(2)
+            multiply_y(3)
+            open_ll(2)
+            add_rows(2, rows=slice(SIDE // 2, SIDE))
+            add_bias(1)
+            sum_squares_on_tensor(2, 0)
+            add_columns(2, 1)
             quantise_weight("q")
+            add_bias(2)
+            add_bias(3)
+            quantise_weight("k")
+            quantise_y(0)
+            project_k(0)
+            project_q(0)
+            quantise_ll(2)
+            ll2_of[3] = head.tile([P, PIX, PACK], BF16, name="ll2", bufs=2, align_bytes=64)
+            sum_squares_on_tensor(3, 0)
+            sum_squares_on_tensor(3, 1)
+            multiply_y(4)
+            multiply_y(5)
+            products(0)
+            add_bias_on_scalar(4)
+            add_bias_on_scalar(5)
             quantise_ll(3)
             multiply_y(6)
             multiply_y(7)
-            quantise_weight("k")
-            quantise_y(0)
-            add_bias(4)
-            add_bias(5)
-            quantise_weight("v")
-            add_bias(6)
-            add_bias(7)
-            quantise_y(1)
+            turn_weight("v")
+            maxima(
+                0,
+                before_last=(
+                    partial(add_bias, 6),
+                    partial(add_bias, 7),
+                    partial(quantise_weight, "v"),
+                    partial(quantise_y, 1),
+                ),
+            )
+            open_e(0)
+            for b, engine in enumerate((nc.vector, nc.gpsimd)):
+                subtract(0, b, engine)
             nc.scalar.copy(out=gamma_pm[:, :, 0], in_=gamma_bf[:])
             nc.scalar.mul(out=gamma_pm[:, :, 1], in_=gamma_bf[:], mul=-1.0)
             nc.scalar.copy(out=beta_pm[:, :, 0], in_=beta_bf[:])
@@ -270,40 +402,10 @@ def tile_merge_pa_kernel(
             nc.scalar.mul(out=minus_slope[:], in_=slope_bf[:], mul=-1.0)
             nc.scalar.add(out=slope_less_one[:], in_=slope_bf[:], add=-1.0)
 
-        z_pair = (z_even, z_odd)
         out_tiles = out.rearrange("b (r a) h w -> a r b (h w)", a=TILES)
-        q_of, v_of, z_max_of, e_of, den_of, num_of = {}, {}, {}, {}, {}, {}
         r_den_of, att_of, sums_of, mean_of, var_of, r_std_of, above_of, below_of = {}, {}, {}, {}, {}, {}, {}, {}
 
-        with tc.tile_pool(name="work", bufs=2) as work, tc.psum_pool(name="banks", bufs=2) as banks:
-
-            def project(name, codes, c, tag, bufs):
-                a, h = divmod(c, HALVES)
-                bank = banks.tile([P, CHUNK], F32, tag=tag, bufs=bufs)
-                rows = slice(a * P, (a + 1) * P)
-                cols = slice(h * CHUNK, (h + 1) * CHUNK)
-                nc.tensor.matmul_mx(
-                    out=bank[:],
-                    lhsT=w_codes[name][:, rows].bitcast(FP8X4),
-                    lhsT_scale=w_scales[name][:, rows],
-                    rhs=codes[:, cols].bitcast(FP8X4),
-                    rhs_scale=y_scales[:, cols],
-                    start=True,
-                    stop=True,
-                )
-                return bank
-
-            def project_q(c):
-                q_of[c] = project("q", y_codes, c, "bank_q", 1)
-
-            def project_k(c):
-                k_bank = project("k", y_codes, c, "bank_k", 1)
-                nc.scalar.copy(
-                    out=k_pads[c % 2][:, 0 : PAIR * SIDE, PAD:], in_=k_bank[:].rearrange("p (r j) -> p r j", j=SIDE)
-                )
-
-            def project_v(c, t, tag="bank_v", bufs=2):
-                v_of[c, t] = project("v", (y_left, y_codes, y_right)[t], c, tag, bufs)
+        with tc.tile_pool(name="work", bufs=2) as work:
 
             def sum_planes(total, blocks, images, projections):
                 for g in range(BLOCKS):
@@ -321,53 +423,9 @@ def tile_merge_pa_kernel(
                                 stop=(d == TAPS - 1),
                             )
 
-            def products(c):
-                k_flat = k_pads[c % 2][:].rearrange("p r w -> p (r w)")
-                width = PAD + SIDE
-                for s, di in enumerate(SHIFTS):
-                    i0, i1 = inside(di)
-                    for t, dj in enumerate(SHIFTS):
-                        k_rows = k_flat[:, PAD + dj : PAD + dj + PAIR * SIDE * width].rearrange(
-                            "p (b i w) -> p b i w", b=PAIR, w=width
-                        )
-                        z = z_pair[c % 2][:, s * 3 + t].rearrange("p b (i j) -> p b i j", j=SIDE)
-                        nc.vector.tensor_tensor(
-                            out=z[:, :, i0:i1],
-                            in0=q_of[c][:].rearrange("p (b i j) -> p b i j", b=PAIR, j=SIDE)[:, :, i0:i1],
-                            in1=k_rows[:, :, i0 + di : i1 + di, 0:SIDE],
-                            op=ALU.mult,
-                        )
-
-            def maxima(c):
-                z_planes = z_pair[c % 2]
-                top = work.tile([P, 4, PAIR, PIX], F32, tag="top")
-                z_max = work.tile([P, PAIR, PIX], F32, tag="z_max")
-                for b in range(PAIR):
-                    nc.vector.tensor_max(out=top[:, :, b], in0=z_planes[:, 0:4, b], in1=z_planes[:, 4:8, b])
-                for b in range(PAIR):
-                    nc.vector.tensor_max(out=top[:, 0:2, b], in0=top[:, 0:2, b], in1=top[:, 2:4, b])
-                for b in range(PAIR):
-                    nc.vector.tensor_max(out=top[:, 0, b], in0=top[:, 0, b], in1=top[:, 1, b])
-                for b in range(PAIR):
-                    nc.vector.tensor_max(out=z_max[:, b], in0=top[:, 0, b], in1=z_planes[:, 8, b])
-                z_max_of[c] = z_max
-
-            def open_e(c):
-                e_of[c] = work.tile([P, TAPS, PAIR, PIX], F32, name="e", bufs=2)
-
-            def subtract(c, b, engine):
-                engine.tensor_tensor(
-                    out=e_of[c][:, :, b],
-                    in0=z_pair[c % 2][:, :, b],
-                    in1=z_max_of[c][:, b].unsqueeze(1).to_broadcast([P, TAPS, PIX]),
-                    op=ALU.subtract,
-                )
-
-            def exponentiate(c, b):
-                nc.scalar.activation(out=e_of[c][:, :, b], in_=e_of[c][:, :, b], func=ACT.Exp)
-
             def open_sum_e(c):
-                den_of[c] = banks.tile([P, BLOCKS, P], F32, name="den_t", bufs=2)
+                total = banks.tile([P, BLOCKS, P], F32, tag="den_t", bufs=2)
+                den_of[c] = total
 
             def sum_e(c, images=range(PAIR), projections=()):
                 blocks = e_of[c][:].rearrange("p d b (f x) -> p d (b f) x", f=2)
@@ -403,7 +461,8 @@ def tile_merge_pa_kernel(
                 for h in range(HALVES):
                     nc.scalar.activation(out=ln_den[:, h], in_=den_of[a * HALVES + h][:], func=ACT.Ln)
                 r_den = work.tile([P, HALVES, BLOCKS, P], F32, tag="r_den")
-                nc.scalar.activation(out=r_den[:], in_=ln_den[:], func=ACT.Exp, scale=-1.0)
+                for h in range(HALVES):
+                    nc.scalar.activation(out=r_den[:, h], in_=ln_den[:, h], func=ACT.Exp, scale=-1.0)
                 r_den_of[a] = r_den
 
             def divide(a, h):
@@ -493,17 +552,11 @@ def tile_merge_pa_kernel(
                 return 0 <= c < CHUNKS
 
             LAST = CHUNKS - 1
-            project_k(0)
-            project_q(0)
             project_k(1)
-            products(0)
             project_q(1)
             project_v(0, 0)
             project_v(0, 1)
-            maxima(0)
-            open_e(0)
-            for b, engine in enumerate((nc.vector, nc.gpsimd)):
-                subtract(0, b, engine)
+            for b in range(PAIR):
                 exponentiate(0, b)
             products(1)
             for r in range(1, CHUNKS):
@@ -512,7 +565,9 @@ def tile_merge_pa_kernel(
                 open_sum_e(r - 1)
                 sum_e(
                     r - 1,
-                    projections=(partial(project_k, r + 1), partial(project_q, r + 1)) if live(r + 1) else (),
+                    projections=(partial(project_k, r + 1), partial(project_q, r + 1))
+                    if live(r + 1)
+                    else (partial(project_v, r - 1, 2, "bank_q", 1),),
                 )
                 if even:
                     reciprocal(a)
@@ -527,12 +582,13 @@ def tile_merge_pa_kernel(
                     affine(a)
                 subtract(r, 1, nc.gpsimd)
                 exponentiate(r, 1)
-                weigh(r - 1, 0, pv)
-                project_v(r - 1, 2)
-                weigh(r - 1, 1, pv)
-                weigh(r - 1, 2, pv)
-                open_sum_pv(r - 1)
-                sum_pv(r - 1, pv, projections=(partial(project_v, r, 0), partial(project_v, r, 1)))
+                if r < LAST:
+                    weigh(r - 1, 0, pv)
+                    project_v(r - 1, 2)
+                    weigh(r - 1, 1, pv)
+                    weigh(r - 1, 2, pv)
+                    open_sum_pv(r - 1)
+                    sum_pv(r - 1, pv, projections=(partial(project_v, r, 0), partial(project_v, r, 1)))
                 if live(r + 1):
                     products(r + 1)
                 if even:
@@ -544,13 +600,22 @@ def tile_merge_pa_kernel(
                         combine(a, h)
 
             a = TILES - 1
-            open_sum_e(LAST)
-            open_sum_pv(LAST)
             pv_last = z_pair[(LAST - 1) % 2]
+            open_sum_pv(LAST - 1)
+            for t in range(len(SHIFTS)):
+                weigh(LAST - 1, t, pv, slice(0, 1))
+            sum_pv(LAST - 1, pv, (0,))
+            open_sum_e(LAST)
+            sum_e(LAST, (0,))
+            for t in range(len(SHIFTS)):
+                weigh(LAST - 1, t, pv, slice(1, 2))
+            project_v(LAST, 0)
+            project_v(LAST, 1)
             project_v(LAST, 2, "bank_q", 1)
+            sum_pv(LAST - 1, pv, (1,))
+            sum_e(LAST, (1,))
+            open_sum_pv(LAST)
             for b in range(PAIR):
-                sum_e(LAST, (b,))
-            for b in range(2):
                 for t in range(len(SHIFTS)):
                     weigh(LAST, t, pv_last, slice(b, b + 1))
                 sum_pv(LAST, pv_last, (b,))

@@ -6,6 +6,7 @@ from concourse.masks import make_identity
 F32 = mybir.dt.float32
 BF16 = mybir.dt.bfloat16
 U32 = mybir.dt.uint32
+I32 = mybir.dt.int32
 U8 = mybir.dt.uint8
 FP8X4 = mybir.dt.float8_e4m3fn_x4
 ALU = mybir.AluOpType
@@ -58,8 +59,8 @@ def tile_merge_pa_kernel(
         y_scales = keep.tile([P, IMAGES * PIX], U8, align_bytes=64)
         y_left = keep.tile([P, IMAGES * PIX], U32, align_bytes=64)
         y_right = keep.tile([P, IMAGES * PIX], U32, align_bytes=64)
-        for words, edge in ((y_left, SIDE - 1), (y_right, 0)):
-            nc.gpsimd.memset(words[:].rearrange("p (r j) -> p r j", j=SIDE)[:, :, edge : edge + 1], 0)
+        for words in (y_left, y_right):
+            nc.gpsimd.memset(words[:], 0)
 
         z_even = keep.tile([P, TAPS, PAIR, PIX], F32)
         z_odd = keep.tile([P, TAPS, PAIR, PIX], F32)
@@ -328,10 +329,14 @@ def tile_merge_pa_kernel(
                     scales=y_scales[:, cols],
                     in_=y_bf[:, cols, :].rearrange("p x t -> p (x t)"),
                 )
-                whole = y_codes[:, cols].rearrange("p (r j) -> p r j", j=SIDE)
+
+            def cut_edges(h, engine):
+                cols = slice(h * CHUNK, (h + 1) * CHUNK)
+                whole = y_codes[:, cols].bitcast(I32).rearrange("p (r j) -> p r j", j=SIDE)
                 for words, kept in ((y_left, slice(0, SIDE - 1)), (y_right, slice(1, SIDE))):
-                    nc.gpsimd.tensor_copy(
-                        out=words[:, cols].rearrange("p (r j) -> p r j", j=SIDE)[:, :, kept], in_=whole[:, :, kept]
+                    engine.tensor_copy(
+                        out=words[:, cols].bitcast(I32).rearrange("p (r j) -> p r j", j=SIDE)[:, :, kept],
+                        in_=whole[:, :, kept],
                     )
 
             turn_weight("c1")
@@ -368,6 +373,7 @@ def tile_merge_pa_kernel(
             add_bias(3)
             quantise_weight("k")
             quantise_y(0)
+            cut_edges(0, nc.gpsimd)
             project_k(0)
             project_q(0)
             quantise_ll(2)
@@ -390,6 +396,7 @@ def tile_merge_pa_kernel(
                     partial(add_bias, 7),
                     partial(quantise_weight, "v"),
                     partial(quantise_y, 1),
+                    partial(cut_edges, 1, nc.vector),
                 ),
             )
             open_e(0)
@@ -531,7 +538,7 @@ def tile_merge_pa_kernel(
                 above_of[a], below_of[a] = above, below
 
             def combine(a, h):
-                result = work.tile([P, CHUNK], F32, tag="result")
+                result = work.tile([P, CHUNK], F32, tag="result", bufs=4)
                 nc.vector.scalar_tensor_tensor(
                     out=result[:],
                     in0=below_of[a][:, h],
@@ -659,7 +666,7 @@ def tile_merge_pa_kernel(
             nc.vector.tensor_scalar(
                 out=n_below[:], in0=n[:], scalar1=0.0, scalar2=slope_less_one[:], op0=ALU.min, op1=ALU.mult
             )
-            result = work.tile([P, CHUNK], F32, tag="result")
+            result = work.tile([P, CHUNK], F32, tag="result", bufs=4)
             nc.vector.tensor_tensor(out=result[:], in0=n[:], in1=n_below[:], op=ALU.add)
             store(a, 1, result)
             combine(a, 0)

@@ -123,7 +123,7 @@ def tile_merge_pa_kernel(
         def project_v(c, t, tag="bank_v", bufs=2):
             v_of[c, t] = project("v", (y_left, y_codes, y_right)[t], c, tag, bufs)
 
-        def products(c):
+        def products(c, q_copy=None):
             k_flat = k_pads[c % 2][:].rearrange("p r w -> p (r w)")
             width = PAD + SIDE
             for s, di in enumerate(SHIFTS):
@@ -133,9 +133,11 @@ def tile_merge_pa_kernel(
                         "p (b i w) -> p b i w", b=PAIR, w=width
                     )
                     z = z_pair[c % 2][:, s * 3 + t].rearrange("p b (i j) -> p b i j", j=SIDE)
-                    nc.vector.tensor_tensor(
+                    shared = s == 0 and q_copy is not None
+                    q = q_copy if shared else q_of[c]
+                    (nc.gpsimd if shared else nc.vector).tensor_tensor(
                         out=z[:, :, i0:i1],
-                        in0=q_of[c][:].rearrange("p (b i j) -> p b i j", b=PAIR, j=SIDE)[:, :, i0:i1],
+                        in0=q[:].rearrange("p (b i j) -> p b i j", b=PAIR, j=SIDE)[:, :, i0:i1],
                         in1=k_rows[:, :, i0 + di : i1 + di, 0:SIDE],
                         op=ALU.mult,
                     )
@@ -144,6 +146,7 @@ def tile_merge_pa_kernel(
             z_planes = z_pair[c % 2]
             top = keep.tile([P, 4, PAIR, PIX], F32, tag="top")
             z_max = keep.tile([P, PAIR, PIX], F32, tag="z_max", bufs=2)
+            z_max_of[c] = z_max
             for b in range(PAIR):
                 nc.vector.tensor_max(out=top[:, :, b], in0=z_planes[:, 0:4, b], in1=z_planes[:, 4:8, b])
             for b in range(PAIR):
@@ -155,7 +158,6 @@ def tile_merge_pa_kernel(
                     for step in before_last:
                         step()
                 nc.vector.tensor_max(out=z_max[:, b], in0=top[:, 0, b], in1=z_planes[:, 8, b])
-            z_max_of[c] = z_max
 
         def open_e(c):
             e = keep.tile([P, TAPS, PAIR, PIX], F32, tag="e", bufs=2)
@@ -376,32 +378,34 @@ def tile_merge_pa_kernel(
             cut_edges(0, nc.gpsimd)
             project_k(0)
             project_q(0)
+            q_copy = head.tile([P, CHUNK], F32, bufs=1)
+            nc.scalar.copy(out=q_copy[:], in_=q_of[0][:])
             quantise_ll(2)
             ll2_of[3] = head.tile([P, PIX, PACK], BF16, name="ll2", bufs=2, align_bytes=64)
             sum_squares_on_tensor(3, 0)
             sum_squares_on_tensor(3, 1)
             multiply_y(4)
             multiply_y(5)
-            products(0)
+            products(0, q_copy)
             add_bias_on_scalar(4)
             add_bias_on_scalar(5)
-            quantise_ll(3)
-            multiply_y(6)
-            multiply_y(7)
             turn_weight("v")
+            open_e(0)
             maxima(
                 0,
                 before_last=(
+                    partial(quantise_ll, 3),
+                    partial(multiply_y, 6),
+                    partial(multiply_y, 7),
+                    partial(subtract, 0, 0, nc.vector),
                     partial(add_bias, 6),
                     partial(add_bias, 7),
-                    partial(quantise_weight, "v"),
                     partial(quantise_y, 1),
+                    partial(quantise_weight, "v"),
                     partial(cut_edges, 1, nc.vector),
                 ),
             )
-            open_e(0)
-            for b, engine in enumerate((nc.vector, nc.gpsimd)):
-                subtract(0, b, engine)
+            subtract(0, 1, nc.gpsimd)
             nc.scalar.copy(out=gamma_pm[:, :, 0], in_=gamma_bf[:])
             nc.scalar.mul(out=gamma_pm[:, :, 1], in_=gamma_bf[:], mul=-1.0)
             nc.scalar.copy(out=beta_pm[:, :, 0], in_=beta_bf[:])
@@ -612,13 +616,13 @@ def tile_merge_pa_kernel(
             for t in range(len(SHIFTS)):
                 weigh(LAST - 1, t, pv, slice(0, 1))
             sum_pv(LAST - 1, pv, (0,))
-            open_sum_e(LAST)
-            sum_e(LAST, (0,))
             for t in range(len(SHIFTS)):
                 weigh(LAST - 1, t, pv, slice(1, 2))
             project_v(LAST, 0)
             project_v(LAST, 1)
             project_v(LAST, 2, "bank_q", 1)
+            open_sum_e(LAST)
+            sum_e(LAST, (0,))
             sum_pv(LAST - 1, pv, (1,))
             sum_e(LAST, (1,))
             open_sum_pv(LAST)

@@ -530,8 +530,8 @@ def tile_merge_pa_kernel(
                         scale=mean_of[a][:],
                         bias=beta_pm[:, a, sign : sign + 1],
                     )
-                above = work.tile([P, HALVES, CHUNK], F32, tag="above")
-                below = work.tile([P, HALVES, CHUNK], F32, tag="below")
+                above = work.tile([P, HALVES, CHUNK], F32, tag="above", bufs=3)
+                below = work.tile([P, HALVES, CHUNK], F32, tag="below", bufs=3)
                 for h in range(HALVES):
                     nc.scalar.activation(
                         out=above[:, h], in_=att_of[a][:, h], func=ACT.Relu, scale=gain[:, 0:1], bias=shift[:, 0:1]
@@ -606,7 +606,7 @@ def tile_merge_pa_kernel(
                     open_att(a)
                     for h in range(HALVES):
                         keep_att(a, h, divide(a, h))
-                elif a >= 0 and r < LAST:
+                elif a == 0:
                     for h in range(HALVES):
                         combine(a, h)
 
@@ -630,8 +630,9 @@ def tile_merge_pa_kernel(
                 for t in range(len(SHIFTS)):
                     weigh(LAST, t, pv_last, slice(b, b + 1))
                 sum_pv(LAST, pv_last, (b,))
-            for h in range(HALVES):
-                combine(a - 1, h)
+            for earlier in (1, 2):
+                for h in range(HALVES):
+                    combine(earlier, h)
             reciprocal(a)
             stats = work.tile([P, HALVES, 6], F32, bufs=1)
             att = work.tile([P, CHUNK], F32, name="att_last", bufs=1)
@@ -657,8 +658,8 @@ def tile_merge_pa_kernel(
                     op0=ALU.mult,
                     op1=ALU.add,
                 )
-            above = work.tile([P, HALVES, CHUNK], F32, tag="above")
-            below = work.tile([P, HALVES, CHUNK], F32, tag="below")
+            above = work.tile([P, HALVES, CHUNK], F32, tag="above", bufs=3)
+            below = work.tile([P, HALVES, CHUNK], F32, tag="below", bufs=3)
             nc.scalar.activation(out=above[:, 0], in_=att[:], func=ACT.Relu, scale=gain[:, 0:1], bias=shift[:, 0:1])
             nc.scalar.activation(out=below[:, 0], in_=att[:], func=ACT.Relu, scale=gain[:, 1:2], bias=shift[:, 1:2])
             above_of[a], below_of[a] = above, below

from functools import partial

import concourse.mybir as mybir
from concourse.masks import make_identity

F32 = mybir.dt.float32
BF16 = mybir.dt.bfloat16
U32 = mybir.dt.uint32
I32 = mybir.dt.int32
U8 = mybir.dt.uint8
FP8X4 = mybir.dt.float8_e4m3fn_x4
ALU = mybir.AluOpType
ACT = mybir.ActivationFunctionType

P = 128
PACK = 4
IMAGES = 4
CHANNELS = 512
SIDE = 16
PIX = SIDE * SIDE
PAIR = 2
CHUNK = PAIR * PIX
PAD = 4
TILES = CHANNELS // P
HALVES = IMAGES // PAIR
CHUNKS = TILES * HALVES
SHIFTS = (-1, 0, 1)
TAPS = len(SHIFTS) * len(SHIFTS)
BLOCKS = CHUNK // P
RUN = 4
BN_EPS = 1e-5
BN_COUNT = IMAGES * PIX

FLOPS = 4 * 2 * CHANNELS * CHANNELS * IMAGES * PIX


def inside(shift):
    return max(0, -shift), SIDE - max(0, shift)


def tile_merge_pa_kernel(
    tc, x, w_c1, b_c1, w_q, w_k, w_v, bn_gamma, bn_beta, prelu_a, out
):
    nc = tc.nc
    weights = {"c1": w_c1, "q": w_q, "k": w_k, "v": w_v}

    with tc.tile_pool(name="keep", bufs=1) as keep, tc.psum_pool(name="banks", bufs=2) as banks, tc.manual_schedule():
        ident = keep.tile([P, P], F32)
        make_identity(nc, ident[:])
        ident_bf = keep.tile([P, P], BF16)
        make_identity(nc, ident_bf[:])

        w_codes = {}
        w_scales = {}
        for name in weights:
            w_codes[name] = keep.tile([P, CHANNELS], U32, name="codes_" + name, align_bytes=64)
            w_scales[name] = keep.tile([P, CHANNELS], U8, name="scales_" + name, align_bytes=64)
        y_codes = keep.tile([P, IMAGES * PIX], U32, align_bytes=64)
        y_scales = keep.tile([P, IMAGES * PIX], U8, align_bytes=64)
        y_left = keep.tile([P, IMAGES * PIX], U32, align_bytes=64)
        y_right = keep.tile([P, IMAGES * PIX], U32, align_bytes=64)
        for words in (y_left, y_right):
            nc.gpsimd.memset(words[:], 0)

        z_even = keep.tile([P, TAPS, PAIR, PIX], F32)
        z_odd = keep.tile([P, TAPS, PAIR, PIX], F32)
        pv = keep.tile([P, TAPS, PAIR, PIX], F32)
        k_pads = [keep.tile([P, PAIR * SIDE + 1, PAD + SIDE], F32, name="k_pad%d" % i) for i in range(2)]
        zeros = keep.tile([P, PAIR * SIDE + 1, PAD], F32)
        nc.vector.memset(zeros[:], 0.0)

        def zero_borders(planes, zero):
            zero(planes[:, 0:3, :, 0 : SIDE + 1])
            zero(planes[:, 3:6, :, 0:1])
            zero(planes[:, 3:6, :, PIX - 1 : PIX])
            zero(planes[:, 6:9, :, PIX - SIDE - 1 : PIX])

        def copy_zeros(border):
            dims = border.shape
            source = zeros[:].rearrange("p r w -> p (r w)")[:, 0 : dims[1] * dims[2] * dims[3]]
            nc.scalar.copy(out=border, in_=source.rearrange("p (a b c) -> p a b c", a=dims[1], b=dims[2]))

        zero_borders(z_even, lambda border: nc.vector.memset(border, 0.0))

        bias_c1 = keep.tile([P, PACK], F32)
        gamma_pm = keep.tile([P, TILES, 2], F32)
        beta_pm = keep.tile([P, TILES, 2], F32)
        minus_slope = keep.tile([P, 1], F32)
        slope_less_one = keep.tile([P, 1], F32)
        minus_half = keep.tile([P, 1], F32)
        nc.gpsimd.memset(minus_half[:], -0.5)
        eps = keep.tile([P, 1], F32)
        nc.gpsimd.memset(eps[:], BN_EPS)

        z_pair = (z_even, z_odd)
        q_of, v_of, z_max_of, e_of, den_of, num_of = {}, {}, {}, {}, {}, {}

        def project(name, codes, c, tag, bufs):
            a, h = divmod(c, HALVES)
            bank = banks.tile([P, CHUNK], F32, tag=tag, bufs=bufs)
            rows = slice(a * P, (a + 1) * P)
            cols = slice(h * CHUNK, (h + 1) * CHUNK)
            nc.tensor.matmul_mx(
                out=bank[:],
                lhsT=w_codes[name][:, rows].bitcast(FP8X4),
                lhsT_scale=w_scales[name][:, rows],
                rhs=codes[:, cols].bitcast(FP8X4),
                rhs_scale=y_scales[:, cols],
                start=True,
                stop=True,
            )
            return bank

        def project_q(c):
            q_of[c] = project("q", y_codes, c, "bank_q", 1)

        def project_k(c):
            k_bank = project("k", y_codes, c, "bank_k", 1)
            nc.scalar.copy(
                out=k_pads[c % 2][:, 0 : PAIR * SIDE, PAD:], in_=k_bank[:].rearrange("p (r j) -> p r j", j=SIDE)
            )

        def project_v(c, t, tag="bank_v", bufs=2):
            v_of[c, t] = project("v", (y_left, y_codes, y_right)[t], c, tag, bufs)

        def products(c, q_copy=None):
            k_flat = k_pads[c % 2][:].rearrange("p r w -> p (r w)")
            width = PAD + SIDE
            for s, di in enumerate(SHIFTS):
                i0, i1 = inside(di)
                for t, dj in enumerate(SHIFTS):
                    k_rows = k_flat[:, PAD + dj : PAD + dj + PAIR * SIDE * width].rearrange(
                        "p (b i w) -> p b i w", b=PAIR, w=width
                    )
                    z = z_pair[c % 2][:, s * 3 + t].rearrange("p b (i j) -> p b i j", j=SIDE)
                    shared = s == 0 and q_copy is not None
                    q = q_copy if shared else q_of[c]
                    (nc.gpsimd if shared else nc.vector).tensor_tensor(
                        out=z[:, :, i0:i1],
                        in0=q[:].rearrange("p (b i j) -> p b i j", b=PAIR, j=SIDE)[:, :, i0:i1],
                        in1=k_rows[:, :, i0 + di : i1 + di, 0:SIDE],
                        op=ALU.mult,
                    )

        def maxima(c, before_last=()):
            z_planes = z_pair[c % 2]
            top = keep.tile([P, 4, PAIR, PIX], F32, tag="top")
            z_max = keep.tile([P, PAIR, PIX], F32, tag="z_max", bufs=2)
            z_max_of[c] = z_max
            for b in range(PAIR):
                nc.vector.tensor_max(out=top[:, :, b], in0=z_planes[:, 0:4, b], in1=z_planes[:, 4:8, b])
            for b in range(PAIR):
                nc.vector.tensor_max(out=top[:, 0:2, b], in0=top[:, 0:2, b], in1=top[:, 2:4, b])
            for b in range(PAIR):
                nc.vector.tensor_max(out=top[:, 0, b], in0=top[:, 0, b], in1=top[:, 1, b])
            for b in range(PAIR):
                if b == PAIR - 1:
                    for step in before_last:
                        step()
                nc.vector.tensor_max(out=z_max[:, b], in0=top[:, 0, b], in1=z_planes[:, 8, b])

        def open_e(c):
            e = keep.tile([P, TAPS, PAIR, PIX], F32, tag="e", bufs=2)
            e_of[c] = e

        def subtract(c, b, engine):
            engine.tensor_tensor(
                out=e_of[c][:, :, b],
                in0=z_pair[c % 2][:, :, b],
                in1=z_max_of[c][:, b].unsqueeze(1).to_broadcast([P, TAPS, PIX]),
                op=ALU.subtract,
            )

        def exponentiate(c, b):
            nc.scalar.activation(out=e_of[c][:, :, b], in_=e_of[c][:, :, b], func=ACT.Exp)

        with tc.tile_pool(name="head", bufs=2) as head:
            x_sb = []
            w_raw = {}

            def load_image(b, parts):
                x_sb.append(head.tile([P, PACK * 4 * PIX], BF16, name="x%d" % b, bufs=1))
                step = PACK * 4 * PIX // parts
                for part in range(parts):
                    cols = slice(part * step, (part + 1) * step)
                    nc.sync.dma_start(
                        out=x_sb[b][:, cols], in_=x[b].rearrange("(p t) h w -> p (t h w)", t=PACK)[:, cols]
                    )

            def load_weight(name):
                w_raw[name] = head.tile([P, TILES * CHANNELS], BF16, name="raw_" + name, bufs=1)
                nc.sync.dma_start(out=w_raw[name][:], in_=weights[name].rearrange("(r a) k -> r (a k)", a=TILES))

            load_image(0, 2)
            load_weight("c1")
            load_image(1, 1)
            b1_bf = head.tile([P, PACK], BF16, bufs=1)
            nc.sync.dma_start(out=b1_bf[:], in_=b_c1.rearrange("(r t) -> r t", t=PACK))
            load_weight("q")
            load_weight("k")
            load_image(2, 1)
            load_image(3, 1)
            load_weight("v")
            gamma_bf = head.tile([P, TILES], BF16, bufs=1)
            nc.sync.dma_start(out=gamma_bf[:], in_=bn_gamma.rearrange("(r a) -> r a", a=TILES))
            beta_bf = head.tile([P, TILES], BF16, bufs=1)
            nc.sync.dma_start(out=beta_bf[:], in_=bn_beta.rearrange("(r a) -> r a", a=TILES))
            slope_bf = head.tile([P, 1], BF16, bufs=1)
            nc.sync.dma_start(out=slope_bf[:], in_=prelu_a.partition_broadcast(P))

            grouped_of = {}

            def turn_weight(name):
                words = w_raw[name][:].bitcast(F32)
                grouped = head.tile([P, TILES * P * PACK], BF16, name="grouped_" + name, bufs=1, align_bytes=64)
                grouped_words = grouped[:].bitcast(F32).rearrange("p (a r u) -> p a r u", a=TILES, u=2)
                for first in range(0, TILES, 2):
                    turned = banks.tile([P, 2, 2, P], F32, tag="den_t", bufs=2)
                    for a in range(2):
                        for u in range(2):
                            row = (first + a) * 2 * P
                            nc.tensor.transpose(
                                turned[:, a, u, :], words[:, row + u : row + 2 * P : 2], ident[:]
                            )
                    nc.scalar.copy(
                        out=grouped_words[:, first : first + 2],
                        in_=turned[:].rearrange("p a u r -> p a r u"),
                    )
                grouped_of[name] = grouped

            def quantise_weight(name):
                nc.vector.quantize_mx(
                    out=w_codes[name][:].bitcast(FP8X4), scales=w_scales[name][:], in_=grouped_of[name][:]
                )

            ll_codes = head.tile([P, IMAGES * PIX], U32, bufs=1, align_bytes=64)
            ll_scales = head.tile([P, IMAGES * PIX], U8, bufs=1, align_bytes=64)
            row_sums_of, ll2_of = {}, {}

            def open_ll(b):
                row_sums_of[b] = head.tile([P, PACK, SIDE, 2 * SIDE], F32, name="row_sums", bufs=2)
                ll2_of[b] = head.tile([P, PIX, PACK], BF16, name="ll2", bufs=2, align_bytes=64)

            def add_rows(b, channels=slice(0, PACK), rows=slice(0, SIDE)):
                x_rows = x_sb[b][:].rearrange("p (t i two w) -> p t i two w", t=PACK, i=SIDE, two=2)
                nc.vector.tensor_tensor(
                    out=row_sums_of[b][:, channels, rows],
                    in0=x_rows[:, channels, rows, 0, :],
                    in1=x_rows[:, channels, rows, 1, :],
                    op=ALU.add,
                )

            def add_columns(b, part):
                pixels = slice(part * P, (part + 1) * P)
                col_pairs = row_sums_of[b][:].rearrange("p t i (j two) -> p t (i j) two", two=2)[:, :, pixels, :]
                col_pairs = col_pairs.rearrange("p t (c i) two -> p c t i two", i=RUN)
                nc.vector.tensor_tensor(
                    out=ll2_of[b][:, pixels, :].rearrange("p (c i) t -> p c t i", i=RUN),
                    in0=col_pairs[:, :, :, :, 0],
                    in1=col_pairs[:, :, :, :, 1],
                    op=ALU.add,
                )

            def sum_squares_on_tensor(b, part):
                rows = slice(part * P // SIDE, (part + 1) * P // SIDE)
                squares = x_sb[b][:].rearrange("p (t i a j c) -> p t i a j c", t=PACK, i=SIDE, a=2, j=SIDE)
                ll_bank = banks.tile([P, PACK, P], F32, tag="bank_v", bufs=2)
                for n in range(4):
                    nc.tensor.matmul(
                        out=ll_bank[:].rearrange("p t (i j) -> p t i j", j=SIDE),
                        lhsT=ident_bf[:],
                        rhs=squares[:, :, rows, n // 2, :, n % 2],
                        start=(n == 0),
                        stop=(n == 3),
                    )
                nc.scalar.copy(
                    out=ll2_of[b][:, part * P : (part + 1) * P, :], in_=ll_bank[:].rearrange("p t x -> p x t")
                )

            def quantise_ll(b):
                cols = slice(b * PIX, (b + 1) * PIX)
                nc.vector.quantize_mx(
                    out=ll_codes[:, cols].bitcast(FP8X4),
                    scales=ll_scales[:, cols],
                    in_=ll2_of[b][:].rearrange("p x t -> p (x t)"),
                )

            y_bf = head.tile([P, IMAGES * PIX, PACK], BF16, bufs=1, align_bytes=64)
            y_bank_of = {}

            def multiply_y(g):
                cols = slice(g * P, (g + 1) * P)
                y_bank = banks.tile([P, PACK, P], F32, tag="num_t", bufs=2)
                for t in range(PACK):
                    rows = slice(t * P, (t + 1) * P)
                    nc.tensor.matmul_mx(
                        out=y_bank[:, t, :],
                        lhsT=w_codes["c1"][:, rows].bitcast(FP8X4),
                        lhsT_scale=w_scales["c1"][:, rows],
                        rhs=ll_codes[:, cols].bitcast(FP8X4),
                        rhs_scale=ll_scales[:, cols],
                        start=True,
                        stop=True,
                    )
                y_bank_of[g] = y_bank

            def add_bias(g):
                nc.vector.scalar_tensor_tensor(
                    out=y_bf[:, g * P : (g + 1) * P, :],
                    in0=y_bank_of[g][:].rearrange("p t x -> p x t"),
                    scalar=0.5,
                    in1=bias_c1[:].unsqueeze(1).to_broadcast([P, P, PACK]),
                    op0=ALU.mult,
                    op1=ALU.add,
                )

            def add_bias_on_scalar(g):
                for t in range(PACK):
                    nc.scalar.activation(
                        out=y_bf[:, g * P : (g + 1) * P, t],
                        in_=y_bank_of[g][:, t, :],
                        func=ACT.Identity,
                        scale=0.5,
                        bias=bias_c1[:, t : t + 1],
                    )

            def quantise_y(h):
                cols = slice(h * CHUNK, (h + 1) * CHUNK)
                nc.vector.quantize_mx(
                    out=y_codes[:, cols].bitcast(FP8X4),
                    scales=y_scales[:, cols],
                    in_=y_bf[:, cols, :].rearrange("p x t -> p (x t)"),
                )

            def cut_edges(h, engine):
                cols = slice(h * CHUNK, (h + 1) * CHUNK)
                whole = y_codes[:, cols].bitcast(I32).rearrange("p (r j) -> p r j", j=SIDE)
                for words, kept in ((y_left, slice(0, SIDE - 1)), (y_right, slice(1, SIDE))):
                    engine.tensor_copy(
                        out=words[:, cols].bitcast(I32).rearrange("p (r j) -> p r j", j=SIDE)[:, :, kept],
                        in_=whole[:, :, kept],
                    )

            turn_weight("c1")
            for k_pad in k_pads:
                nc.scalar.copy(out=k_pad[:, :, 0:PAD], in_=zeros[:])
            for planes in (z_odd, pv):
                zero_borders(planes, copy_zeros)
            nc.scalar.copy(out=bias_c1[:], in_=b1_bf[:])
            for b in range(2):
                open_ll(b)
                add_rows(b, channels=slice(0, 2))
                if b == 1:
                    quantise_ll(0)
                add_rows(b, channels=slice(2, 4))
                if b == 1:
                    quantise_weight("c1")
                    turn_weight("q")
                    multiply_y(0)
                    multiply_y(1)
                    turn_weight("k")
                add_columns(b, 0)
                add_columns(b, 1)
            add_bias(0)
            quantise_ll(1)
            multiply_y(2)
            multiply_y(3)
            open_ll(2)
            add_rows(2, rows=slice(SIDE // 2, SIDE))
            add_bias(1)
            sum_squares_on_tensor(2, 0)
            add_columns(2, 1)
            quantise_weight("q")
            add_bias(2)
            add_bias(3)
            quantise_weight("k")
            quantise_y(0)
            cut_edges(0, nc.gpsimd)
            project_k(0)
            project_q(0)
            q_copy = head.tile([P, CHUNK], F32, bufs=1)
            nc.scalar.copy(out=q_copy[:], in_=q_of[0][:])
            quantise_ll(2)
            ll2_of[3] = head.tile([P, PIX, PACK], BF16, name="ll2", bufs=2, align_bytes=64)
            sum_squares_on_tensor(3, 0)
            sum_squares_on_tensor(3, 1)
            multiply_y(4)
            multiply_y(5)
            products(0, q_copy)
            add_bias_on_scalar(4)
            add_bias_on_scalar(5)
            turn_weight("v")
            open_e(0)
            maxima(
                0,
                before_last=(
                    partial(quantise_ll, 3),
                    partial(multiply_y, 6),
                    partial(multiply_y, 7),
                    partial(subtract, 0, 0, nc.vector),
                    partial(add_bias, 6),
                    partial(add_bias, 7),
                    partial(quantise_y, 1),
                    partial(quantise_weight, "v"),
                    partial(cut_edges, 1, nc.vector),
                ),
            )
            subtract(0, 1, nc.gpsimd)
            nc.scalar.copy(out=gamma_pm[:, :, 0], in_=gamma_bf[:])
            nc.scalar.mul(out=gamma_pm[:, :, 1], in_=gamma_bf[:], mul=-1.0)
            nc.scalar.copy(out=beta_pm[:, :, 0], in_=beta_bf[:])
            nc.scalar.mul(out=beta_pm[:, :, 1], in_=beta_bf[:], mul=-1.0)
            nc.scalar.mul(out=minus_slope[:], in_=slope_bf[:], mul=-1.0)
            nc.scalar.add(out=slope_less_one[:], in_=slope_bf[:], add=-1.0)

        out_tiles = out.rearrange("b (r a) h w -> a r b (h w)", a=TILES)
        r_den_of, att_of, sums_of, mean_of, var_of, r_std_of, above_of, below_of = {}, {}, {}, {}, {}, {}, {}, {}

        with tc.tile_pool(name="work", bufs=2) as work:

            def sum_planes(total, blocks, images, projections):
                for g in range(BLOCKS):
                    if g == 1:
                        for projection in projections:
                            projection()
                    if g // (BLOCKS // PAIR) in images:
                        for d in range(TAPS):
                            nc.tensor.matmul(
                                out=total[:, g, :],
                                lhsT=blocks[:, d, g, :],
                                rhs=ident[:],
                                is_transpose=True,
                                start=(d == 0),
                                stop=(d == TAPS - 1),
                            )

            def open_sum_e(c):
                total = banks.tile([P, BLOCKS, P], F32, tag="den_t", bufs=2)
                den_of[c] = total

            def sum_e(c, images=range(PAIR), projections=()):
                blocks = e_of[c][:].rearrange("p d b (f x) -> p d (b f) x", f=2)
                sum_planes(den_of[c], blocks, images, projections)

            def weigh(c, t, planes, images=slice(0, PAIR)):
                v_maps = v_of[c, t][:].rearrange("p (b x) -> p b x", b=PAIR)
                for s, di in enumerate(SHIFTS):
                    i0, i1 = inside(di)
                    shift = SIDE * di + SHIFTS[t]
                    first = max(SIDE * i0, -shift)
                    last = min(SIDE * i1, PIX - shift)
                    nc.vector.tensor_tensor(
                        out=planes[:, s * 3 + t, images, first:last],
                        in0=v_maps[:, images, first + shift : last + shift],
                        in1=e_of[c][:, s * 3 + t, images, first:last],
                        op=ALU.mult,
                    )

            def pixel_bank():
                bank = banks.tile([P, BLOCKS, P], F32, tag="num_t", bufs=2)
                return bank

            def open_sum_pv(c):
                num_of[c] = pixel_bank()

            def sum_pv(c, planes, images=range(PAIR), projections=()):
                blocks = planes[:].rearrange("p d b (f x) -> p d (b f) x", f=2)
                sum_planes(num_of[c], blocks, images, projections)

            def reciprocal(a):
                ln_den = work.tile([P, HALVES, BLOCKS, P], F32, tag="ln_den", bufs=1)
                for h in range(HALVES):
                    nc.scalar.activation(out=ln_den[:, h], in_=den_of[a * HALVES + h][:], func=ACT.Ln)
                r_den = work.tile([P, HALVES, BLOCKS, P], F32, tag="r_den")
                for h in range(HALVES):
                    nc.scalar.activation(out=r_den[:, h], in_=ln_den[:, h], func=ACT.Exp, scale=-1.0)
                r_den_of[a] = r_den

            def divide(a, h):
                att_t = work.tile([P, BLOCKS, P], F32, tag="att_t")
                nc.vector.tensor_mul(out=att_t[:], in0=num_of[a * HALVES + h][:], in1=r_den_of[a][:, h])
                att_bank = pixel_bank()
                for g in range(BLOCKS):
                    nc.tensor.transpose(att_bank[:, g, :], att_t[:, g, :], ident[:])
                return att_bank[:].rearrange("p g x -> p (g x)")

            def open_att(a):
                att_of[a] = work.tile([P, HALVES, CHUNK], F32, name="att", bufs=2)
                sums_of[a] = work.tile([P, HALVES], F32, name="att_sums", bufs=2)

            def keep_att(a, h, att):
                nc.scalar.activation(
                    out=att_of[a][:, h, :], in_=att, func=ACT.Copy, accum_out=sums_of[a][:, h : h + 1]
                )

            def statistics(a):
                parts = work.tile([P, HALVES], F32, tag="parts")
                nc.scalar.activation(out=parts[:], in_=sums_of[a][:], func=ACT.Copy, scale=-1.0 / BN_COUNT)
                minus_mean = work.tile([P, 1], F32, tag="minus_mean")
                nc.scalar.activation(out=minus_mean[:], in_=parts[:, 0:1], func=ACT.Identity, bias=parts[:, 1:2])
                squares = work.tile([P, HALVES * CHUNK], F32, tag="squares", bufs=1)
                sum_squares = work.tile([P, 1], F32, tag="sum_squares")
                nc.scalar.activation(
                    out=squares[:],
                    in_=att_of[a][:].rearrange("p h x -> p (h x)"),
                    func=ACT.Square,
                    bias=minus_mean[:],
                    accum_out=sum_squares[:],
                )
                var_eps = work.tile([P, 1], F32, tag="var_eps")
                nc.scalar.activation(
                    out=var_eps[:], in_=sum_squares[:], func=ACT.Identity, scale=1.0 / BN_COUNT, bias=eps[:]
                )
                mean_of[a], var_of[a] = minus_mean, var_eps

            def rsqrt(a):
                r_std = work.tile([P, 1], F32, tag="r_std")
                nc.gpsimd.tensor_tensor(out=r_std[:], in0=var_of[a][:], in1=minus_half[:], op=ALU.pow)
                r_std_of[a] = r_std

            def affine(a):
                gain = work.tile([P, 2], F32, tag="gain")
                nc.scalar.activation(out=gain[:], in_=gamma_pm[:, a, :], func=ACT.Copy, scale=r_std_of[a][:])
                shift = work.tile([P, 2], F32, tag="shift")
                for sign in range(2):
                    nc.scalar.activation(
                        out=shift[:, sign : sign + 1],
                        in_=gain[:, sign : sign + 1],
                        func=ACT.Identity,
                        scale=mean_of[a][:],
                        bias=beta_pm[:, a, sign : sign + 1],
                    )
                above = work.tile([P, HALVES, CHUNK], F32, tag="above", bufs=3)
                below = work.tile([P, HALVES, CHUNK], F32, tag="below", bufs=3)
                for h in range(HALVES):
                    nc.scalar.activation(
                        out=above[:, h], in_=att_of[a][:, h], func=ACT.Relu, scale=gain[:, 0:1], bias=shift[:, 0:1]
                    )
                    nc.scalar.activation(
                        out=below[:, h], in_=att_of[a][:, h], func=ACT.Relu, scale=gain[:, 1:2], bias=shift[:, 1:2]
                    )
                above_of[a], below_of[a] = above, below

            def combine(a, h):
                result = work.tile([P, CHUNK], F32, tag="result", bufs=4)
                nc.vector.scalar_tensor_tensor(
                    out=result[:],
                    in0=below_of[a][:, h],
                    scalar=minus_slope[:],
                    in1=above_of[a][:, h],
                    op0=ALU.mult,
                    op1=ALU.add,
                )
                store(a, h, result)

            def store(a, h, result):
                nc.sync.dma_start(
                    out=out_tiles[a][:, h * PAIR : (h + 1) * PAIR, :],
                    in_=result[:].rearrange("p (b x) -> p b x", b=PAIR),
                )

            def live(c):
                return 0 <= c < CHUNKS

            LAST = CHUNKS - 1
            project_k(1)
            project_q(1)
            project_v(0, 0)
            project_v(0, 1)
            for b in range(PAIR):
                exponentiate(0, b)
            products(1)
            for r in range(1, CHUNKS):
                a = r // 2 - 1
                even = r % 2 == 0
                open_sum_e(r - 1)
                sum_e(
                    r - 1,
                    projections=(partial(project_k, r + 1), partial(project_q, r + 1))
                    if live(r + 1)
                    else (partial(project_v, r - 1, 2, "bank_q", 1),),
                )
                if even:
                    reciprocal(a)
                elif a >= 0:
                    statistics(a)
                maxima(r)
                open_e(r)
                subtract(r, 0, nc.gpsimd if r < LAST else nc.vector)
                exponentiate(r, 0)
                if not even and a >= 0:
                    rsqrt(a)
                    affine(a)
                subtract(r, 1, nc.gpsimd)
                exponentiate(r, 1)
                if r < LAST:
                    weigh(r - 1, 0, pv)
                    project_v(r - 1, 2)
                    weigh(r - 1, 1, pv)
                    weigh(r - 1, 2, pv)
                    open_sum_pv(r - 1)
                    sum_pv(r - 1, pv, projections=(partial(project_v, r, 0), partial(project_v, r, 1)))
                if live(r + 1):
                    products(r + 1)
                if even:
                    open_att(a)
                    for h in range(HALVES):
                        keep_att(a, h, divide(a, h))
                elif a == 0:
                    for h in range(HALVES):
                        combine(a, h)

            a = TILES - 1
            pv_last = z_pair[(LAST - 1) % 2]
            open_sum_pv(LAST - 1)
            for t in range(len(SHIFTS)):
                weigh(LAST - 1, t, pv, slice(0, 1))
            sum_pv(LAST - 1, pv, (0,))
            for t in range(len(SHIFTS)):
                weigh(LAST - 1, t, pv, slice(1, 2))
            project_v(LAST, 0)
            project_v(LAST, 1)
            project_v(LAST, 2, "bank_q", 1)
            open_sum_e(LAST)
            sum_e(LAST, (0,))
            sum_pv(LAST - 1, pv, (1,))
            sum_e(LAST, (1,))
            open_sum_pv(LAST)
            for b in range(PAIR):
                for t in range(len(SHIFTS)):
                    weigh(LAST, t, pv_last, slice(b, b + 1))
                sum_pv(LAST, pv_last, (b,))
            for earlier in (1, 2):
                for h in range(HALVES):
                    combine(earlier, h)
            reciprocal(a)
            stats = work.tile([P, HALVES, 6], F32, bufs=1)
            att = work.tile([P, CHUNK], F32, name="att_last", bufs=1)
            att_banks = [divide(a, h) for h in range(HALVES)]
            for h in range(HALVES):
                nc.vector.bn_stats(out=stats[:, h, :], in_=att_banks[h])
            nc.scalar.copy(out=att[:], in_=att_banks[0])
            mean_var = work.tile([P, 2], F32, bufs=1)
            nc.vector.bn_aggr(out=mean_var[:], in_=stats[:].rearrange("p h s -> p (h s)"))
            var_eps = work.tile([P, 1], F32, name="var_eps_last", bufs=1)
            nc.vector.tensor_scalar_add(out=var_eps[:], in0=mean_var[:, 1:2], scalar1=BN_EPS)
            var_of[a] = var_eps
            rsqrt(a)
            gain = work.tile([P, 2], F32, name="gain_last", bufs=1)
            nc.vector.tensor_scalar_mul(out=gain[:], in0=gamma_pm[:, a, :], scalar1=r_std_of[a][:])
            shift = work.tile([P, 2], F32, name="shift_last", bufs=1)
            for sign in range(2):
                nc.vector.scalar_tensor_tensor(
                    out=shift[:, sign : sign + 1],
                    in0=mean_var[:, 0:1],
                    scalar=gain[:, 1 - sign : 2 - sign],
                    in1=beta_pm[:, a, sign : sign + 1],
                    op0=ALU.mult,
                    op1=ALU.add,
                )
            above = work.tile([P, HALVES, CHUNK], F32, tag="above", bufs=3)
            below = work.tile([P, HALVES, CHUNK], F32, tag="below", bufs=3)
            nc.scalar.activation(out=above[:, 0], in_=att[:], func=ACT.Relu, scale=gain[:, 0:1], bias=shift[:, 0:1])
            nc.scalar.activation(out=below[:, 0], in_=att[:], func=ACT.Relu, scale=gain[:, 1:2], bias=shift[:, 1:2])
            above_of[a], below_of[a] = above, below
            n = work.tile([P, CHUNK], F32, name="n_last", bufs=1)
            nc.vector.tensor_scalar(
                out=n[:], in0=att_banks[1], scalar1=gain[:, 0:1], scalar2=shift[:, 0:1], op0=ALU.mult, op1=ALU.add
            )
            n_below = work.tile([P, CHUNK], F32, name="n_below", bufs=1)
            nc.vector.tensor_scalar(
                out=n_below[:], in0=n[:], scalar1=0.0, scalar2=slope_less_one[:], op0=ALU.min, op1=ALU.mult
            )
            result = work.tile([P, CHUNK], F32, tag="result", bufs=4)
            nc.vector.tensor_tensor(out=result[:], in0=n[:], in1=n_below[:], op=ALU.add)
            store(a, 1, result)
            combine(a, 0)
